import numpy as np
import ml_dtypes


def mxq(x, axis, fmt="e4m3"):
    dtype, down = {"e4m3": (ml_dtypes.float8_e4m3fn, 7), "e5m2": (ml_dtypes.float8_e5m2, 14)}[fmt]
    v = np.moveaxis(np.asarray(x, np.float32).astype(ml_dtypes.bfloat16).astype(np.float64), axis, -1)
    blocks = v.reshape(v.shape[:-1] + (-1, 32))
    amax = np.abs(blocks).max(-1, keepdims=True)
    byte = np.maximum(np.where(amax > 0, np.frexp(amax)[1] - 1 + 127, 0) - down, 1)
    scale = np.exp2(byte - 127.0)
    codes = (blocks / scale).astype(np.float32).astype(dtype).astype(np.float64)
    return np.moveaxis((codes * scale).reshape(v.shape), -1, axis)


WIDE = False


def mx_kscale(k):
    if not WIDE:
        return np.ones(k)
    levels = np.array([18, -18])
    if k % 512:
        return np.exp2(np.random.permutation(np.resize(levels, k // 32))).repeat(32)
    a = np.empty((k // 512, 16))
    for p in range(k // 512):
        a[p, :8] = np.random.permutation(np.resize(levels, 8))
        for g in range(8):
            far = levels[np.abs(levels - a[p, g]) >= 10]
            a[p, g + 8] = far[np.random.randint(len(far))]
    return np.exp2(a.ravel()).repeat(32)


BF16 = ml_dtypes.bfloat16


def bf(x):
    return np.asarray(x, np.float32).astype(BF16)


def f64(x):
    return np.asarray(x).astype(np.float64)


N, C, T, V, H, O = 32, 1024, 16, 25, 512, 1024


def setup_inputs():
    s = mx_kscale(N * T).reshape(N, T)
    u = mx_kscale(O)
    v = mx_kscale(H)
    wscale = 0.7 * np.sqrt(V / C)
    xm0 = bf(np.random.standard_normal((N, C, T)) / np.sqrt(V))
    Wq0 = bf(np.random.standard_normal((H, C)) * wscale)
    bq = bf(np.random.standard_normal(H) * 0.3)
    Wk0 = bf(np.random.standard_normal((H, C)) * wscale)
    bk = bf(np.random.standard_normal(H) * 0.3)
    Wr0 = bf(np.random.standard_normal((O, H)) / np.sqrt(H))
    br = bf(np.random.standard_normal(O) * 0.3)
    g = np.random.standard_normal((N, O, T, T)) * np.exp2(np.random.randint(-6, 1, (N, 1, T, 1)))
    q = f64(Wq0) @ f64(xm0) + f64(bq)[None, :, None]
    k = f64(Wk0) @ f64(xm0) + f64(bk)[None, :, None]
    return {
        "xm": bf(f64(xm0) * s[:, None, :]),
        "Wq": bf(f64(Wq0) / v[:, None]),
        "bq": bq,
        "Wk": bf(f64(Wk0) / v[:, None]),
        "bk": bk,
        "Wr": bf(f64(Wr0) * v[None, :] / u[:, None]),
        "br": br,
        "q": np.asarray(q, np.float32),
        "k": np.asarray(k, np.float32),
        "grad_out": bf(g * u[None, :, None, None] / s[:, None, :, None]),
    }


def reference(xm, Wq, bq, Wk, bk, Wr, br, q, k, grad_out):
    go = f64(grad_out).transpose(0, 2, 3, 1).reshape(N * T * T, O)
    dd = mxq(go, 1, "e5m2") @ mxq(f64(Wr), 0, "e4m3")
    d = np.tanh(f64(q)[:, :, :, None] - f64(k)[:, :, None, :])
    dp = dd.reshape(N, T, T, H).transpose(0, 3, 1, 2) * (1.0 - d * d)
    dq = dp.sum(axis=3)
    dk = -dp.sum(axis=2)
    dqt = dq.transpose(0, 2, 1).reshape(N * T, H)
    dkt = dk.transpose(0, 2, 1).reshape(N * T, H)
    dz1 = np.concatenate([dqt, dkt], axis=1)
    w1 = np.concatenate([f64(Wq), f64(Wk)], axis=0)
    xt = f64(xm).transpose(0, 2, 1).reshape(N * T, C)
    dx = mxq(dz1, 1, "e5m2") @ mxq(w1, 0, "e4m3")
    dwq = mxq(dz1[:, :H], 0, "e5m2").T @ mxq(xt, 0, "e4m3")
    return dx.reshape(N, T, C).transpose(0, 2, 1), dwq

@@ -1,0 +1,392 @@
+from contextlib import ExitStack
+
+import concourse.mybir as mybir
+from concourse.masks import make_identity
+
+N, C, T, H, O = 32, 1024, 16, 512, 1024
+FLOPS = 2 * N * T * T * O * H + 2 * N * T * 2 * H * C + 2 * N * T * H * C
+BYTES = 2 * (N * C * T + 2 * H * C + O * H + N * O * T * T) + 4 * (2 * N * H * T + N * C * T + H * C)
+
+F32 = mybir.dt.float32
+BF16 = mybir.dt.bfloat16
+U32 = mybir.dt.uint32
+U8 = mybir.dt.uint8
+E4 = mybir.dt.float8_e4m3fn_x4
+E5 = mybir.dt.float8_e5m2_x4
+ACT = mybir.ActivationFunctionType
+ALU = mybir.AluOpType
+
+P = 128
+BANK = 512
+GROUP = 8
+GROUPS = N // GROUP
+STEPS = 8
+ALL_STEPS = GROUPS * STEPS
+LEAD = 7
+RAW_BUFS = 6
+SCALAR_SAMPLE = 3
+
+
+def tile_ta_block_pa_v_kernel(tc, xm, Wq, bq, Wk, bk, Wr, br, q, k, grad_out, out_0, out_1):
+    nc = tc.nc
+    with ExitStack() as ctx:
+        sb = ctx.enter_context(tc.tile_pool(name="sb", bufs=1))
+        ps = ctx.enter_context(tc.psum_pool(name="ps", bufs=1))
+        ctx.enter_context(tc.manual_schedule())
+
+        def sbuf(tag, width, dtype, bufs=1):
+            return sb.tile([P, width], dtype, tag=tag, name=tag, bufs=bufs, align_bytes=64)
+
+        bank_bufs = {"diff": 2, "dd": 2, "sums": 4}
+
+        def bank(tag):
+            return ps.tile([P, BANK], F32, tag=tag, name=tag, bufs=bank_bufs[tag])
+
+        def copy(engine, out, in_):
+            if engine == "scalar":
+                nc.scalar.copy(out=out, in_=in_)
+            else:
+                nc.vector.tensor_copy(out=out, in_=in_)
+
+        def quantize(fmt, codes, scales, first, values):
+            cols = slice(first, first + values.shape[1] // 4)
+            nc.vector.quantize_mx(out=codes[:, cols].bitcast(fmt), scales=scales[:, cols], in_=values)
+
+        sources = [Wr[512 * s : 512 * (s + 1), :].rearrange("(p j) h -> p j h", j=4) for s in range(2)]
+        sources.extend(grad_out[n].rearrange("(s p j) g t -> p s (j g t)", s=2, j=4) for n in range(N))
+        for w in (Wq, Wk):
+            rows = w.rearrange("(p j) c -> p j c", j=4)
+            sources.extend(rows[:, :, 512 * half : 512 * (half + 1)] for half in range(2))
+        sources.extend(xm[16 * half : 16 * (half + 1)].rearrange("n (m c) f -> m n (c f)", c=8) for half in range(2))
+        WR_RAW, GO_RAW, W1_RAW, XM_RAW = 0, 2, 2 + N, 6 + N
+        raw = []
+
+        def load_next():
+            if len(raw) < len(sources):
+                src = sources[len(raw)]
+                dst = sbuf("raw", 2048, BF16, RAW_BUFS)
+                nc.sync.dma_start(out=dst[:].rearrange("p (a b) -> p a b", a=src.shape[1]), in_=src)
+                raw.append(dst)
+
+        q_raw, k_raw = {}, {}
+
+        def load_saved(grp):
+            for name, src, tiles, bufs in (("k_raw", k, k_raw, 1), ("q_raw", q, q_raw, 2)):
+                tiles[grp] = sbuf(name, 512, F32, bufs)
+                nc.sync.dma_start(
+                    out=tiles[grp][:].rearrange("p (n w) -> p n w", n=GROUP),
+                    in_=src[GROUP * grp : GROUP * (grp + 1)].rearrange("n (m h) f -> m n (h f)", h=4),
+                )
+
+        load_saved(0)
+        for first_loads in range(RAW_BUFS):
+            load_next()
+
+        ident = sbuf("ident", P, F32)
+        make_identity(nc, ident[:])
+        zeros = sbuf("zeros", BANK, BF16)
+        nc.vector.memset(zeros[:], 0.0)
+        warm = sbuf("warm", 16, F32)
+        nc.scalar.activation(out=warm[:], in_=zeros[:, 0:16], func=ACT.Tanh)
+        pick = sbuf("pick", 64, F32)
+        nc.vector.tensor_reduce(
+            out=pick[:, 0:32].rearrange("p (n g) -> p n g", g=4),
+            in_=ident[:].rearrange("p (g n t) -> p n g t", g=4, t=4),
+            axis=mybir.AxisListType.X,
+            op=ALU.add,
+        )
+        nc.vector.tensor_reduce(
+            out=pick[:, 32:64], in_=ident[:].rearrange("p (g x) -> p x g", g=4), axis=mybir.AxisListType.X, op=ALU.add
+        )
+        nc.vector.tensor_scalar(out=pick[:, 0:32], in0=pick[:, 0:32], scalar1=-1.0, scalar2=None, op0=ALU.mult)
+
+        wr_codes, wr_scales = sbuf("wr_codes", 1024, U32), sbuf("wr_scales", 1024, U8)
+        w1_codes, w1_scales = sbuf("w1_codes", 2048, U32), sbuf("w1_scales", 2048, U8)
+        xm_codes, xm_scales = sbuf("xm_codes", 1024, U32), sbuf("xm_scales", 1024, U8)
+        dz_codes, dz_scales = sbuf("dz_codes", 1024, U32), sbuf("dz_scales", 1024, U8)
+        dqt_codes, dqt_scales = sbuf("dqt_codes", 512, U32), sbuf("dqt_scales", 512, U8)
+        dq_pairs = sbuf("dq_pairs", 2048, BF16)
+        dq_tokens = sbuf("dq_tokens", 2048, BF16)
+
+        k_neg, k_wide, q_wide, squares, woven, go_codes, go_scales, dd_banks, dp_neg, sums, dz = ({} for d in range(11))
+
+        def spread(step):
+            grp, r = divmod(step, STEPS)
+            if r == 0:
+                k_neg[grp] = sbuf("k_neg", 512, F32)
+                nc.vector.tensor_scalar(
+                    out=k_neg[grp][:].rearrange("p (a n t) -> p a n t", n=GROUP, t=4),
+                    in0=k_raw[grp][:].rearrange("p (n a t) -> p a n t", n=GROUP, t=4),
+                    scalar1=-1.0,
+                    scalar2=None,
+                    op0=ALU.mult,
+                )
+            if r % 2 == 0:
+                gq = r // 2
+                q_wide[grp, gq] = sbuf("q_wide", 512, F32, 2)
+                src = q_raw[grp][:].rearrange("p (n h g s) -> p h g n s", h=4, g=4, s=4)[:, :, :, :, gq : gq + 1]
+                nc.vector.tensor_copy(
+                    out=q_wide[grp, gq][:].rearrange("p (h g n t) -> p h g n t", h=4, g=4, t=4),
+                    in_=src.to_broadcast([P, 4, 4, GROUP, 4]),
+                )
+            if r < 2:
+                k_wide[grp, r] = sbuf("k_wide", 1024, F32, 3)
+                src = k_neg[grp][:].rearrange("p (h a o x) -> p a h o x", h=4, a=4, o=1)[:, 2 * r : 2 * r + 2]
+                nc.vector.tensor_copy(
+                    out=k_wide[grp, r][:].rearrange("p (a h g x) -> p a h g x", a=2, h=4, g=4),
+                    in_=src.to_broadcast([P, 2, 4, 4, 32]),
+                )
+
+        def differences(step):
+            grp, r = divmod(step, STEPS)
+            squares[step] = sbuf("squares", 2 * BANK, F32, LEAD + 1)
+            banks = []
+            for u in range(2):
+                diff = bank("diff")
+                for h in range(4):
+                    cols = slice(P * h, P * (h + 1))
+                    k_cols = slice(BANK * u + P * h, BANK * u + P * (h + 1))
+                    nc.tensor.matmul(diff[:, cols], lhsT=q_wide[grp, r // 2][:, cols], rhs=ident[:], start=True, stop=False, is_transpose=True)
+                    nc.tensor.matmul(diff[:, cols], lhsT=k_wide[grp, r % 2][:, k_cols], rhs=ident[:], start=False, stop=True, is_transpose=True)
+                banks.append(diff)
+            for u in range(2):
+                nc.scalar.activation(out=squares[step][:, BANK * u : BANK * (u + 1)], in_=banks[u][:], func=ACT.Tanh)
+
+        def square(step):
+            nc.scalar.activation(out=squares[step][:], in_=squares[step][:], func=ACT.Square)
+
+        def weave(sample, engine):
+            grp, n = divmod(sample, GROUP)
+            if n == 0:
+                woven[grp] = sbuf("woven", 16384, BF16, 2)
+            copy(
+                engine,
+                woven[grp][:].rearrange("p (l s g n t j) -> p n s g l j t", s=2, g=4, n=GROUP, t=4, j=4)[:, n],
+                raw[GO_RAW + sample][:].rearrange("p (s j g l t) -> p s g l j t", s=2, j=4, g=4, t=4),
+            )
+            load_next()
+
+        def quantize_go(step):
+            grp, r = divmod(step, STEPS)
+            go_codes[step], go_scales[step] = sbuf("go_codes", 512, U32, 3), sbuf("go_scales", 512, U8, 3)
+            quantize(E5, go_codes[step], go_scales[step], 0, woven[grp][:, 2048 * r : 2048 * (r + 1)])
+
+        def multiply(step):
+            for u in range(2):
+                dd = bank("dd")
+                for s in range(2):
+                    cols = slice(P * (2 * u + s), P * (2 * u + s + 1))
+                    w_cols = slice(BANK * s, BANK * (s + 1))
+                    nc.tensor.matmul_mx(
+                        out=dd[:],
+                        lhsT=go_codes[step][:, cols].bitcast(E5),
+                        lhsT_scale=go_scales[step][:, cols],
+                        rhs=wr_codes[:, w_cols].bitcast(E4),
+                        rhs_scale=wr_scales[:, w_cols],
+                        start=(s == 0),
+                        stop=(s == 1),
+                    )
+                dd_banks[step, u] = dd
+            for u in range(2):
+                dp_neg[step, u] = sbuf("dp_neg", BANK, F32, 4)
+                nc.vector.scalar_tensor_tensor(
+                    out=dp_neg[step, u][:],
+                    in0=squares[step][:, BANK * u : BANK * (u + 1)],
+                    scalar=1.0,
+                    in1=dd_banks[step, u][:],
+                    op0=ALU.subtract,
+                    op1=ALU.mult,
+                )
+
+        def add_up(step):
+            grp, r = divmod(step, STEPS)
+            if r == 0:
+                sums[grp] = [bank("sums"), bank("sums")]
+                for acc in sums[grp]:
+                    nc.tensor.matmul(acc[:], lhsT=zeros[:, 0:P], rhs=zeros[:], start=True, stop=False)
+            for u in range(2):
+                gq, tq = r // 2, 2 * (r % 2) + u
+                for h in range(4):
+                    lo, hi = 8 * (h % 2) + gq, 8 * (h % 2) + 4 + tq
+                    nc.tensor.matmul(
+                        sums[grp][h // 2][:].rearrange("p (r c) -> p r c", c=32)[:, lo : hi + 1 : hi - lo, :],
+                        lhsT=dp_neg[step, u][:, P * h : P * (h + 1)],
+                        rhs=pick[:].rearrange("p (r c) -> p r c", c=32),
+                        start=False,
+                        stop=(r == STEPS - 1 and u == 1 and h % 2 == 1),
+                    )
+
+        def round_sums(grp, engines):
+            dz[grp] = sbuf("dz", 1024, BF16, 2)
+            for b in range(2):
+                copy(
+                    engines[b],
+                    dq_pairs[:].rearrange("p (h u c e) -> p h u c e", h=4, u=2, e=2)[:, 2 * b : 2 * b + 2, :, 32 * grp : 32 * (grp + 1), :],
+                    sums[grp][b][:].rearrange("p (h a u e c) -> p a h u c e", h=2, a=2, u=2, e=2)[:, 0],
+                )
+            for b in range(2):
+                copy(
+                    engines[b],
+                    dz[grp][:].rearrange("p (s c g j) -> p s c g j", s=2, g=4, j=4)[:, 0, :, :, 2 * b : 2 * b + 2],
+                    sums[grp][b][:].rearrange("p (h a g c) -> p a c g h", h=2, a=2, g=4)[:, 0],
+                )
+                copy(
+                    engines[b],
+                    dz[grp][:].rearrange("p (s n a t j) -> p s n a t j", s=2, a=4, t=4, j=4)[:, 1, :, :, :, 2 * b : 2 * b + 2],
+                    sums[grp][b][:].rearrange("p (h s a n t) -> p s n a t h", h=2, s=2, a=4, t=4)[:, 1],
+                )
+
+        def quantize_dz(grp, s):
+            quantize(E5, dz_codes, dz_scales, BANK * s + P * grp, dz[grp][:, BANK * s : BANK * (s + 1)])
+
+        def turn_words(engine, dst, src, pair):
+            turned = bank("diff")
+            for i in range(4):
+                cols = slice(P * (4 * pair + i), P * (4 * pair + i + 1))
+                nc.tensor.transpose(turned[:, P * i : P * (i + 1)], src[:].bitcast(F32)[:, cols], ident[:])
+            copy(
+                engine,
+                dst[:].bitcast(F32)[:, BANK * pair : BANK * (pair + 1)].rearrange("p (c m u) -> p c m u", c=2, u=2),
+                turned[:].rearrange("p (c u m) -> p c m u", c=2, u=2),
+            )
+
+        staged = {}
+
+        def weave_w1(s, half):
+            if half == 0:
+                staged["w1", s] = sbuf("staged", 4096, BF16, 3)
+            for a in range(2):
+                nc.scalar.copy(
+                    out=staged["w1", s][:].rearrange("p (a c f m j) -> p a f m c j", a=2, c=4, f=2, j=4)[:, a, half],
+                    in_=raw[W1_RAW + 2 * s + half][:].rearrange("p (j m a c) -> p a m c j", j=4, a=2, c=4)[:, a],
+                )
+
+        def sort_xm(half):
+            if half == 0:
+                staged["xm_words"] = sbuf("staged", 4096, BF16, 3)
+            nc.vector.tensor_copy(
+                out=staged["xm_words"][:].bitcast(F32).rearrange("p (c u a n f) -> p a c u n f", u=2, a=2, n=16, f=4)[:, half],
+                in_=raw[XM_RAW + half][:].bitcast(F32).rearrange("p (n c f u) -> p c u n f", c=8, f=4, u=2),
+            )
+
+        staged["wr"] = sbuf("staged", 4096, BF16, 3)
+        spread(0)
+        for step in range(LEAD):
+            if step < 2:
+                nc.scalar.copy(
+                    out=staged["wr"][:].rearrange("p (s h m j) -> p s m h j", s=2, h=4, j=4)[:, step],
+                    in_=raw[WR_RAW + step][:].rearrange("p (j m h) -> p m h j", j=4, h=4),
+                )
+                load_next()
+            differences(step)
+            spread(step + 1)
+            weave(step, "vector")
+            if step in (2, 3):
+                s = step - 2
+                quantize(E4, wr_codes, wr_scales, BANK * s, staged["wr"][:, 2048 * s : 2048 * (s + 1)])
+            if step == 1:
+                load_saved(1)
+        weave(GROUP - 1, "vector")
+        square(0)
+        weave(GROUP, "vector")
+        quantize_go(0)
+
+        for step in range(ALL_STEPS):
+            multiply(step)
+            if step > 0:
+                add_up(step - 1)
+                if step % STEPS == 0:
+                    round_sums(step // STEPS - 1, ("scalar", "scalar"))
+            ahead = step + LEAD
+            if ahead < ALL_STEPS:
+                differences(ahead)
+            if step + 1 < ALL_STEPS:
+                square(step + 1)
+                quantize_go(step + 1)
+            if ahead + 1 < ALL_STEPS:
+                spread(ahead + 1)
+                if (ahead + 1) % STEPS == 1 and (ahead + 1) // STEPS + 1 < GROUPS:
+                    load_saved((ahead + 1) // STEPS + 1)
+            if step > STEPS and step % STEPS == 1:
+                for s in range(2):
+                    quantize_dz(step // STEPS - 1, s)
+            sample = step + GROUP + 1
+            if sample < N:
+                weave(sample, "scalar" if sample % GROUP == SCALAR_SAMPLE else "vector")
+            late = step - (N - GROUP - 1)
+            if late in (2, 4):
+                s = late // 2 - 1
+                quantize(E4, w1_codes, w1_scales, 1024 * s, staged["w1", s][:])
+            if 0 <= late < 4:
+                weave_w1(late // 2, late % 2)
+            if late in (0, 1):
+                sort_xm(late)
+            if late == 3:
+                staged["xm"] = sbuf("woven", 4096, BF16, 2)
+            if late in (3, 4):
+                for pair in range(2):
+                    turn_words("scalar", staged["xm"], staged["xm_words"], 2 * (late - 3) + pair)
+            if late in (5, 6):
+                half = late - 5
+                quantize(E4, xm_codes, xm_scales, BANK * half, staged["xm"][:, 2048 * half : 2048 * (half + 1)])
+
+        add_up(ALL_STEPS - 1)
+        round_sums(GROUPS - 1, ("scalar", "vector"))
+        turn_words("scalar", dq_tokens, dq_pairs, 0)
+        quantize_dz(GROUPS - 1, 0)
+        turn_words("vector", dq_tokens, dq_pairs, 1)
+        quantize_dz(GROUPS - 1, 1)
+        quantize(E5, dqt_codes, dqt_scales, 0, dq_tokens[:])
+
+        dwq = sbuf("woven", 4096, F32, 2)
+        dx = sbuf("woven", 4096, F32, 2)
+        tags = ("dd", "dd", "sums", "sums", "diff", "diff", "sums", "sums")
+        jobs = [("dx", 0), ("dx", 1)] + [("dwq", i) for i in range(8)] + [("dx", c) for c in range(2, 8)]
+        for count, (kind, i) in enumerate(jobs):
+            acc = bank(tags[count % 8])
+            engine = ("scalar", "vector")[count % 2]
+            if kind == "dx":
+                for s in range(2):
+                    cols = slice(1024 * s + P * i, 1024 * s + P * (i + 1))
+                    z_cols = slice(BANK * s, BANK * (s + 1))
+                    nc.tensor.matmul_mx(
+                        out=acc[:],
+                        lhsT=w1_codes[:, cols].bitcast(E4),
+                        lhsT_scale=w1_scales[:, cols],
+                        rhs=dz_codes[:, z_cols].bitcast(E5),
+                        rhs_scale=dz_scales[:, z_cols],
+                        start=(s == 0),
+                        stop=(s == 1),
+                    )
+                copy(
+                    engine,
+                    dx[:].rearrange("p (n c f) -> p c n f", c=8, f=T)[:, i],
+                    acc[:].rearrange("p (n f) -> p n f", f=T),
+                )
+            else:
+                h, half = divmod(i, 2)
+                cols = slice(P * h, P * (h + 1))
+                x_cols = slice(BANK * half, BANK * (half + 1))
+                nc.tensor.matmul_mx(
+                    out=acc[:],
+                    lhsT=dqt_codes[:, cols].bitcast(E5),
+                    lhsT_scale=dqt_scales[:, cols],
+                    rhs=xm_codes[:, x_cols].bitcast(E4),
+                    rhs_scale=xm_scales[:, x_cols],
+                    start=True,
+                    stop=True,
+                )
+                copy(
+                    engine,
+                    dwq[:].rearrange("p (h m a c) -> p h a m c", h=4, a=2, c=4)[:, h, half],
+                    acc[:].rearrange("p (c m) -> p m c", c=4),
+                )
+                if half == 1:
+                    nc.sync.dma_start(
+                        out=out_1.rearrange("(m h) c -> m h c", h=4)[:, h, :], in_=dwq[:, C * h : C * (h + 1)]
+                    )
+        for part in range(4):
+            nc.sync.dma_start(
+                out=out_0[8 * part : 8 * (part + 1)].rearrange("n (m c) f -> m n (c f)", c=8),
+                in_=dx[:, 1024 * part : 1024 * (part + 1)].rearrange("p (n w) -> p n w", n=8),
+            )

@@ -24,7 +24,7 @@ STEPS = 8
 ALL_STEPS = GROUPS * STEPS
 LEAD = 7
 RAW_BUFS = 6
-SCALAR_SAMPLE = 3
+VECTOR_DIFF_EVERY = 4
 
 
 def tile_ta_block_pa_v_kernel(tc, xm, Wq, bq, Wk, bk, Wr, br, q, k, grad_out, out_0, out_1):
@@ -33,11 +33,12 @@ def tile_ta_block_pa_v_kernel(tc, xm, Wq, bq, Wk, bk, Wr, br, q, k, grad_out, ou
         sb = ctx.enter_context(tc.tile_pool(name="sb", bufs=1))
         ps = ctx.enter_context(tc.psum_pool(name="ps", bufs=1))
         ctx.enter_context(tc.manual_schedule())
+        ctx.enter_context(nc.allow_low_precision(reason="the sums are float32; their store is dz1's one rounding to bfloat16"))
 
         def sbuf(tag, width, dtype, bufs=1):
             return sb.tile([P, width], dtype, tag=tag, name=tag, bufs=bufs, align_bytes=64)
 
-        bank_bufs = {"diff": 2, "dd": 2, "sums": 4}
+        bank_bufs = {"diff": 2, "dd": 2, "dq": 2, "dk": 2}
 
         def bank(tag):
             return ps.tile([P, BANK], F32, tag=tag, name=tag, bufs=bank_bufs[tag])
@@ -84,86 +85,90 @@ def tile_ta_block_pa_v_kernel(tc, xm, Wq, bq, Wk, bk, Wr, br, q, k, grad_out, ou
 
         ident = sbuf("ident", P, F32)
         make_identity(nc, ident[:])
-        zeros = sbuf("zeros", BANK, BF16)
-        nc.vector.memset(zeros[:], 0.0)
         warm = sbuf("warm", 16, F32)
-        nc.scalar.activation(out=warm[:], in_=zeros[:, 0:16], func=ACT.Tanh)
-        pick = sbuf("pick", 64, F32)
-        nc.vector.tensor_reduce(
-            out=pick[:, 0:32].rearrange("p (n g) -> p n g", g=4),
-            in_=ident[:].rearrange("p (g n t) -> p n g t", g=4, t=4),
-            axis=mybir.AxisListType.X,
-            op=ALU.add,
-        )
-        nc.vector.tensor_reduce(
-            out=pick[:, 32:64], in_=ident[:].rearrange("p (g x) -> p x g", g=4), axis=mybir.AxisListType.X, op=ALU.add
-        )
-        nc.vector.tensor_scalar(out=pick[:, 0:32], in0=pick[:, 0:32], scalar1=-1.0, scalar2=None, op0=ALU.mult)
+        nc.vector.memset(warm[:, 0:8], 0.0)
+        nc.scalar.activation(out=warm[:, 8:16], in_=warm[:, 0:8], func=ACT.Tanh)
 
         wr_codes, wr_scales = sbuf("wr_codes", 1024, U32), sbuf("wr_scales", 1024, U8)
         w1_codes, w1_scales = sbuf("w1_codes", 2048, U32), sbuf("w1_scales", 2048, U8)
         xm_codes, xm_scales = sbuf("xm_codes", 1024, U32), sbuf("xm_scales", 1024, U8)
         dz_codes, dz_scales = sbuf("dz_codes", 1024, U32), sbuf("dz_scales", 1024, U8)
         dqt_codes, dqt_scales = sbuf("dqt_codes", 512, U32), sbuf("dqt_scales", 512, U8)
+        for s in range(2):
+            last_group = slice(BANK * (s + 1) - P, BANK * (s + 1))
+            nc.gpsimd.memset(dz_codes[:, last_group], 0)
+            nc.gpsimd.memset(dz_scales[:, last_group], 0)
         dq_pairs = sbuf("dq_pairs", 2048, BF16)
         dq_tokens = sbuf("dq_tokens", 2048, BF16)
 
-        k_neg, k_wide, q_wide, squares, woven, go_codes, go_scales, dd_banks, dp_neg, sums, dz = ({} for d in range(11))
+        k_wide, q_wide, squares, woven, go_codes, go_scales, dp_neg, dq_sums, dk_sums, dz = ({} for d in range(10))
 
         def spread(step):
-            grp, r = divmod(step, STEPS)
-            if r == 0:
-                k_neg[grp] = sbuf("k_neg", 512, F32)
+            grp, gq = divmod(step, STEPS)
+            if gq == 0:
+                k_wide[grp] = sbuf("k_wide", 2 * BANK, F32, 2)
+                for tq in range(2):
+                    src = k_raw[grp][:].rearrange("p (n h a o t) -> p a h o n t", h=4, a=2, o=1, t=8)[:, tq]
+                    nc.vector.tensor_copy(
+                        out=k_wide[grp][:, BANK * tq : BANK * (tq + 1)].rearrange("p (h g n t) -> p h g n t", h=4, g=2, t=8),
+                        in_=src.to_broadcast([P, 4, 2, GROUP, 8]),
+                    )
+            src = q_raw[grp][:].rearrange("p (n h g s) -> p h g n s", h=4, g=2, s=8)[:, :, :, :, gq : gq + 1]
+            src = src.to_broadcast([P, 4, 2, GROUP, 8])
+            q_wide[step] = sbuf("q_wide", 2 * BANK, F32, 2)
+            if step % VECTOR_DIFF_EVERY == VECTOR_DIFF_EVERY - 1:
+                for tq in range(2):
+                    cols = slice(BANK * tq, BANK * (tq + 1))
+                    nc.vector.tensor_tensor(
+                        out=q_wide[step][:, cols].rearrange("p (h g n t) -> p h g n t", h=4, g=2, t=8),
+                        in0=k_wide[grp][:, cols].rearrange("p (h g n t) -> p h g n t", h=4, g=2, t=8),
+                        in1=src,
+                        op=ALU.subtract,
+                    )
+            else:
                 nc.vector.tensor_scalar(
-                    out=k_neg[grp][:].rearrange("p (a n t) -> p a n t", n=GROUP, t=4),
-                    in0=k_raw[grp][:].rearrange("p (n a t) -> p a n t", n=GROUP, t=4),
+                    out=q_wide[step][:, 0:BANK].rearrange("p (h g n t) -> p h g n t", h=4, g=2, t=8),
+                    in0=src,
                     scalar1=-1.0,
                     scalar2=None,
                     op0=ALU.mult,
                 )
-            if r % 2 == 0:
-                gq = r // 2
-                q_wide[grp, gq] = sbuf("q_wide", 512, F32, 2)
-                src = q_raw[grp][:].rearrange("p (n h g s) -> p h g n s", h=4, g=4, s=4)[:, :, :, :, gq : gq + 1]
-                nc.vector.tensor_copy(
-                    out=q_wide[grp, gq][:].rearrange("p (h g n t) -> p h g n t", h=4, g=4, t=4),
-                    in_=src.to_broadcast([P, 4, 4, GROUP, 4]),
-                )
-            if r < 2:
-                k_wide[grp, r] = sbuf("k_wide", 1024, F32, 3)
-                src = k_neg[grp][:].rearrange("p (h a o x) -> p a h o x", h=4, a=4, o=1)[:, 2 * r : 2 * r + 2]
-                nc.vector.tensor_copy(
-                    out=k_wide[grp, r][:].rearrange("p (a h g x) -> p a h g x", a=2, h=4, g=4),
-                    in_=src.to_broadcast([P, 2, 4, 4, 32]),
-                )
+
+        def add_turned(out, block, start, stop):
+            nc.tensor.matmul(out, lhsT=block, rhs=ident[:], start=start, stop=stop, is_transpose=True)
 
         def differences(step):
-            grp, r = divmod(step, STEPS)
+            grp = step // STEPS
             squares[step] = sbuf("squares", 2 * BANK, F32, LEAD + 1)
             banks = []
-            for u in range(2):
+            for tq in range(2):
                 diff = bank("diff")
                 for h in range(4):
                     cols = slice(P * h, P * (h + 1))
-                    k_cols = slice(BANK * u + P * h, BANK * u + P * (h + 1))
-                    nc.tensor.matmul(diff[:, cols], lhsT=q_wide[grp, r // 2][:, cols], rhs=ident[:], start=True, stop=False, is_transpose=True)
-                    nc.tensor.matmul(diff[:, cols], lhsT=k_wide[grp, r % 2][:, k_cols], rhs=ident[:], start=False, stop=True, is_transpose=True)
+                    tile_cols = slice(BANK * tq + P * h, BANK * tq + P * (h + 1))
+                    if step % VECTOR_DIFF_EVERY == VECTOR_DIFF_EVERY - 1:
+                        add_turned(diff[:, cols], q_wide[step][:, tile_cols], True, True)
+                    else:
+                        add_turned(diff[:, cols], q_wide[step][:, cols], True, False)
+                        add_turned(diff[:, cols], k_wide[grp][:, tile_cols], False, True)
                 banks.append(diff)
-            for u in range(2):
-                nc.scalar.activation(out=squares[step][:, BANK * u : BANK * (u + 1)], in_=banks[u][:], func=ACT.Tanh)
+            for tq in range(2):
+                nc.scalar.activation(out=squares[step][:, BANK * tq : BANK * (tq + 1)], in_=banks[tq][:], func=ACT.Tanh)
 
         def square(step):
             nc.scalar.activation(out=squares[step][:], in_=squares[step][:], func=ACT.Square)
 
-        def weave(sample, engine):
+        def weave(sample, engines):
             grp, n = divmod(sample, GROUP)
             if n == 0:
                 woven[grp] = sbuf("woven", 16384, BF16, 2)
-            copy(
-                engine,
-                woven[grp][:].rearrange("p (l s g n t j) -> p n s g l j t", s=2, g=4, n=GROUP, t=4, j=4)[:, n],
-                raw[GO_RAW + sample][:].rearrange("p (s j g l t) -> p s g l j t", s=2, j=4, g=4, t=4),
-            )
+            dst = woven[grp][:].rearrange("p (l s g n t j) -> p n s g l t j", s=2, g=2, n=GROUP, t=8, j=4)[:, n]
+            src = raw[GO_RAW + sample][:].rearrange("p (s j g l t) -> p s g l t j", s=2, j=4, g=2, t=8)
+            if engines[0] == engines[1]:
+                copy(engines[0], dst, src)
+            else:
+                for s in range(2):
+                    copy(engines[s], dst[:, s], src[:, s])
             load_next()
 
         def quantize_go(step):
@@ -172,6 +177,7 @@ def tile_ta_block_pa_v_kernel(tc, xm, Wq, bq, Wk, bk, Wr, br, q, k, grad_out, ou
             quantize(E5, go_codes[step], go_scales[step], 0, woven[grp][:, 2048 * r : 2048 * (r + 1)])
 
         def multiply(step):
+            dd_banks = []
             for u in range(2):
                 dd = bank("dd")
                 for s in range(2):
@@ -186,55 +192,59 @@ def tile_ta_block_pa_v_kernel(tc, xm, Wq, bq, Wk, bk, Wr, br, q, k, grad_out, ou
                         start=(s == 0),
                         stop=(s == 1),
                     )
-                dd_banks[step, u] = dd
+                dd_banks.append(dd)
             for u in range(2):
                 dp_neg[step, u] = sbuf("dp_neg", BANK, F32, 4)
                 nc.vector.scalar_tensor_tensor(
                     out=dp_neg[step, u][:],
                     in0=squares[step][:, BANK * u : BANK * (u + 1)],
                     scalar=1.0,
-                    in1=dd_banks[step, u][:],
+                    in1=dd_banks[u][:],
                     op0=ALU.subtract,
                     op1=ALU.mult,
                 )
 
         def add_up(step):
-            grp, r = divmod(step, STEPS)
-            if r == 0:
-                sums[grp] = [bank("sums"), bank("sums")]
-                for acc in sums[grp]:
-                    nc.tensor.matmul(acc[:], lhsT=zeros[:, 0:P], rhs=zeros[:], start=True, stop=False)
-            for u in range(2):
-                gq, tq = r // 2, 2 * (r % 2) + u
+            grp, gq = divmod(step, STEPS)
+            dq_sums[step] = bank("dq")
+            if gq == 0:
+                dk_sums[grp] = [bank("dk"), bank("dk")]
+            for tq in range(2):
                 for h in range(4):
-                    lo, hi = 8 * (h % 2) + gq, 8 * (h % 2) + 4 + tq
-                    nc.tensor.matmul(
-                        sums[grp][h // 2][:].rearrange("p (r c) -> p r c", c=32)[:, lo : hi + 1 : hi - lo, :],
-                        lhsT=dp_neg[step, u][:, P * h : P * (h + 1)],
-                        rhs=pick[:].rearrange("p (r c) -> p r c", c=32),
-                        start=False,
-                        stop=(r == STEPS - 1 and u == 1 and h % 2 == 1),
+                    cols = slice(P * h, P * (h + 1))
+                    add_turned(dq_sums[step][:, cols], dp_neg[step, tq][:, cols], tq == 0 and h == 0, tq == 1 and h == 3)
+            for tq in range(2):
+                for h in range(4):
+                    cols = slice(P * h, P * (h + 1))
+                    add_turned(
+                        dk_sums[grp][tq][:, cols], dp_neg[step, tq][:, cols], gq == 0 and h == 0, gq == STEPS - 1 and h == 3
                     )
 
-        def round_sums(grp, engines):
-            dz[grp] = sbuf("dz", 1024, BF16, 2)
-            for b in range(2):
-                copy(
-                    engines[b],
-                    dq_pairs[:].rearrange("p (h u c e) -> p h u c e", h=4, u=2, e=2)[:, 2 * b : 2 * b + 2, :, 32 * grp : 32 * (grp + 1), :],
-                    sums[grp][b][:].rearrange("p (h a u e c) -> p a h u c e", h=2, a=2, u=2, e=2)[:, 0],
-                )
-            for b in range(2):
-                copy(
-                    engines[b],
-                    dz[grp][:].rearrange("p (s c g j) -> p s c g j", s=2, g=4, j=4)[:, 0, :, :, 2 * b : 2 * b + 2],
-                    sums[grp][b][:].rearrange("p (h a g c) -> p a c g h", h=2, a=2, g=4)[:, 0],
-                )
-                copy(
-                    engines[b],
-                    dz[grp][:].rearrange("p (s n a t j) -> p s n a t j", s=2, a=4, t=4, j=4)[:, 1, :, :, :, 2 * b : 2 * b + 2],
-                    sums[grp][b][:].rearrange("p (h s a n t) -> p s n a t h", h=2, s=2, a=4, t=4)[:, 1],
-                )
+        def round_dq(step):
+            grp, gq = divmod(step, STEPS)
+            if gq == 0:
+                dz[grp] = sbuf("dz", 1024, BF16, 2)
+            nc.vector.tensor_reduce(
+                out=dz[grp][:, 0:BANK].rearrange("p (n g s h) -> p s n g h", g=2, s=8, h=4)[:, gq],
+                in_=dq_sums[step][:].rearrange("p (h g n t) -> p n g h t", h=4, g=2, t=8),
+                axis=mybir.AxisListType.X,
+                op=ALU.add,
+                negate=True,
+            )
+
+        def round_dk(grp, tq):
+            nc.vector.tensor_reduce(
+                out=dz[grp][:, BANK : 2 * BANK].rearrange("p (n a t h) -> p a n t h", a=2, t=8, h=4)[:, tq],
+                in_=dk_sums[grp][tq][:].rearrange("p (h g n t) -> p n t h g", h=4, g=2, t=8),
+                axis=mybir.AxisListType.X,
+                op=ALU.add,
+            )
+
+        def pair_dq(grp):
+            nc.scalar.copy(
+                out=dq_pairs[:].rearrange("p (h u c e) -> p h u c e", h=4, u=2, e=2)[:, :, :, 32 * grp : 32 * (grp + 1), :],
+                in_=dz[grp][:, 0:BANK].rearrange("p (c u e h) -> p h u c e", u=2, e=2, h=4),
+            )
 
         def quantize_dz(grp, s):
             quantize(E5, dz_codes, dz_scales, BANK * s + P * grp, dz[grp][:, BANK * s : BANK * (s + 1)])
@@ -269,6 +279,56 @@ def tile_ta_block_pa_v_kernel(tc, xm, Wq, bq, Wk, bk, Wr, br, q, k, grad_out, ou
                 in_=raw[XM_RAW + half][:].bitcast(F32).rearrange("p (n c f u) -> p c u n f", c=8, f=4, u=2),
             )
 
+        def multiply_dx(c, tag, engine, groups):
+            acc = bank(tag)
+            for s in range(2):
+                cols = slice(1024 * s + P * c, 1024 * s + P * (c + 1))
+                z_cols = slice(BANK * s, BANK * (s + 1))
+                nc.tensor.matmul_mx(
+                    out=acc[:],
+                    lhsT=w1_codes[:, cols].bitcast(E4),
+                    lhsT_scale=w1_scales[:, cols],
+                    rhs=dz_codes[:, z_cols].bitcast(E5),
+                    rhs_scale=dz_scales[:, z_cols],
+                    start=(s == 0),
+                    stop=(s == 1),
+                )
+            samples = slice(GROUP * groups.start, GROUP * groups.stop)
+            copy(
+                engine,
+                staged["dx"][:].rearrange("p (n c f) -> p c n f", c=8, f=T)[:, c, samples],
+                acc[:].rearrange("p (n f) -> p n f", f=T)[:, samples],
+            )
+
+        def store_dx(grp):
+            nc.sync.dma_start(
+                out=out_0[GROUP * grp : GROUP * (grp + 1)].rearrange("n (m c) f -> m n (c f)", c=8),
+                in_=staged["dx"][:, 1024 * grp : 1024 * (grp + 1)].rearrange("p (n w) -> p n w", n=GROUP),
+            )
+
+        def multiply_dwq(h, half, tag, engine):
+            acc = bank(tag)
+            cols = slice(P * h, P * (h + 1))
+            x_cols = slice(BANK * half, BANK * (half + 1))
+            nc.tensor.matmul_mx(
+                out=acc[:],
+                lhsT=dqt_codes[:, cols].bitcast(E5),
+                lhsT_scale=dqt_scales[:, cols],
+                rhs=xm_codes[:, x_cols].bitcast(E4),
+                rhs_scale=xm_scales[:, x_cols],
+                start=True,
+                stop=True,
+            )
+            copy(
+                engine,
+                staged["dwq"][:].rearrange("p (h m a c) -> p h a m c", h=4, a=2, c=4)[:, h, half],
+                acc[:].rearrange("p (c m) -> p m c", c=4),
+            )
+            if half == 1:
+                nc.sync.dma_start(
+                    out=out_1.rearrange("(m h) c -> m h c", h=4)[:, h, :], in_=staged["dwq"][:, C * h : C * (h + 1)]
+                )
+
         staged["wr"] = sbuf("staged", 4096, BF16, 3)
         spread(0)
         for step in range(LEAD):
@@ -280,23 +340,21 @@ def tile_ta_block_pa_v_kernel(tc, xm, Wq, bq, Wk, bk, Wr, br, q, k, grad_out, ou
                 load_next()
             differences(step)
             spread(step + 1)
-            weave(step, "vector")
+            weave(step, ("vector", "vector"))
             if step in (2, 3):
                 s = step - 2
                 quantize(E4, wr_codes, wr_scales, BANK * s, staged["wr"][:, 2048 * s : 2048 * (s + 1)])
             if step == 1:
                 load_saved(1)
-        weave(GROUP - 1, "vector")
+        weave(GROUP - 1, ("vector", "vector"))
         square(0)
-        weave(GROUP, "vector")
         quantize_go(0)
+        weave(GROUP, ("scalar", "scalar"))
 
         for step in range(ALL_STEPS):
             multiply(step)
             if step > 0:
                 add_up(step - 1)
-                if step % STEPS == 0:
-                    round_sums(step // STEPS - 1, ("scalar", "scalar"))
             ahead = step + LEAD
             if ahead < ALL_STEPS:
                 differences(ahead)
@@ -308,11 +366,17 @@ def tile_ta_block_pa_v_kernel(tc, xm, Wq, bq, Wk, bk, Wr, br, q, k, grad_out, ou
                 if (ahead + 1) % STEPS == 1 and (ahead + 1) // STEPS + 1 < GROUPS:
                     load_saved((ahead + 1) // STEPS + 1)
             if step > STEPS and step % STEPS == 1:
+                pair_dq(step // STEPS - 1)
                 for s in range(2):
                     quantize_dz(step // STEPS - 1, s)
             sample = step + GROUP + 1
             if sample < N:
-                weave(sample, "scalar" if sample % GROUP == SCALAR_SAMPLE else "vector")
+                weave(sample, ("vector", "scalar"))
+            if step > 0:
+                round_dq(step - 1)
+                if step % STEPS == 0:
+                    for tq in range(2):
+                        round_dk(step // STEPS - 1, tq)
             late = step - (N - GROUP - 1)
             if late in (2, 4):
                 s = late // 2 - 1
@@ -322,71 +386,41 @@ def tile_ta_block_pa_v_kernel(tc, xm, Wq, bq, Wk, bk, Wr, br, q, k, grad_out, ou
             if late in (0, 1):
                 sort_xm(late)
             if late == 3:
-                staged["xm"] = sbuf("woven", 4096, BF16, 2)
+                staged["xm"] = sbuf("staged", 4096, BF16, 3)
             if late in (3, 4):
                 for pair in range(2):
                     turn_words("scalar", staged["xm"], staged["xm_words"], 2 * (late - 3) + pair)
             if late in (5, 6):
                 half = late - 5
                 quantize(E4, xm_codes, xm_scales, BANK * half, staged["xm"][:, 2048 * half : 2048 * (half + 1)])
+            if late == 5:
+                staged["dx"] = sbuf("woven", 4096, F32, 2)
+            if late >= 5:
+                for c in range(2 * (late - 5), 2 * (late - 4)):
+                    multiply_dx(c, "diff", "scalar", range(GROUPS - 1))
+        for grp in range(GROUPS - 1):
+            store_dx(grp)
 
         add_up(ALL_STEPS - 1)
-        round_sums(GROUPS - 1, ("scalar", "vector"))
+        last = GROUPS - 1
+        round_dq(ALL_STEPS - 1)
+        pair_dq(last)
+        round_dk(last, 0)
+        quantize_dz(last, 0)
+        round_dk(last, 1)
         turn_words("scalar", dq_tokens, dq_pairs, 0)
-        quantize_dz(GROUPS - 1, 0)
-        turn_words("vector", dq_tokens, dq_pairs, 1)
-        quantize_dz(GROUPS - 1, 1)
-        quantize(E5, dqt_codes, dqt_scales, 0, dq_tokens[:])
+        turn_words("scalar", dq_tokens, dq_pairs, 1)
+        quantize_dz(last, 1)
+        for pair in range(2):
+            quantize(E5, dqt_codes, dqt_scales, 256 * pair, dq_tokens[:, 1024 * pair : 1024 * (pair + 1)])
 
-        dwq = sbuf("woven", 4096, F32, 2)
-        dx = sbuf("woven", 4096, F32, 2)
-        tags = ("dd", "dd", "sums", "sums", "diff", "diff", "sums", "sums")
-        jobs = [("dx", 0), ("dx", 1)] + [("dwq", i) for i in range(8)] + [("dx", c) for c in range(2, 8)]
+        staged["dwq"] = sbuf("woven", 4096, F32, 2)
+        tags = ("dd", "dd", "dq", "dq", "dk", "dk", "diff", "diff")
+        jobs = [("dx", c) for c in range(2)] + [("dwq", i) for i in range(8)] + [("dx", c) for c in range(2, 8)]
         for count, (kind, i) in enumerate(jobs):
-            acc = bank(tags[count % 8])
             engine = ("scalar", "vector")[count % 2]
             if kind == "dx":
-                for s in range(2):
-                    cols = slice(1024 * s + P * i, 1024 * s + P * (i + 1))
-                    z_cols = slice(BANK * s, BANK * (s + 1))
-                    nc.tensor.matmul_mx(
-                        out=acc[:],
-                        lhsT=w1_codes[:, cols].bitcast(E4),
-                        lhsT_scale=w1_scales[:, cols],
-                        rhs=dz_codes[:, z_cols].bitcast(E5),
-                        rhs_scale=dz_scales[:, z_cols],
-                        start=(s == 0),
-                        stop=(s == 1),
-                    )
-                copy(
-                    engine,
-                    dx[:].rearrange("p (n c f) -> p c n f", c=8, f=T)[:, i],
-                    acc[:].rearrange("p (n f) -> p n f", f=T),
-                )
+                multiply_dx(i, tags[count % 8], engine, range(last, GROUPS))
             else:
-                h, half = divmod(i, 2)
-                cols = slice(P * h, P * (h + 1))
-                x_cols = slice(BANK * half, BANK * (half + 1))
-                nc.tensor.matmul_mx(
-                    out=acc[:],
-                    lhsT=dqt_codes[:, cols].bitcast(E5),
-                    lhsT_scale=dqt_scales[:, cols],
-                    rhs=xm_codes[:, x_cols].bitcast(E4),
-                    rhs_scale=xm_scales[:, x_cols],
-                    start=True,
-                    stop=True,
-                )
-                copy(
-                    engine,
-                    dwq[:].rearrange("p (h m a c) -> p h a m c", h=4, a=2, c=4)[:, h, half],
-                    acc[:].rearrange("p (c m) -> p m c", c=4),
-                )
-                if half == 1:
-                    nc.sync.dma_start(
-                        out=out_1.rearrange("(m h) c -> m h c", h=4)[:, h, :], in_=dwq[:, C * h : C * (h + 1)]
-                    )
-        for part in range(4):
-            nc.sync.dma_start(
-                out=out_0[8 * part : 8 * (part + 1)].rearrange("n (m c) f -> m n (c f)", c=8),
-                in_=dx[:, 1024 * part : 1024 * (part + 1)].rearrange("p (n w) -> p n w", n=8),
-            )
+                multiply_dwq(i // 2, i % 2, tags[count % 8], engine)
+        store_dx(last)

@@ -11,8 +11,8 @@ F32 = mybir.dt.float32
 BF16 = mybir.dt.bfloat16
 U32 = mybir.dt.uint32
 U8 = mybir.dt.uint8
-E4 = mybir.dt.float8_e4m3fn_x4
-E5 = mybir.dt.float8_e5m2_x4
+E4M3 = mybir.dt.float8_e4m3fn_x4
+E5M2 = mybir.dt.float8_e5m2_x4
 ACT = mybir.ActivationFunctionType
 ALU = mybir.AluOpType
 
@@ -21,10 +21,12 @@ BANK = 512
 GROUP = 8
 GROUPS = N // GROUP
 STEPS = 8
+TILES = 2 * STEPS
 ALL_STEPS = GROUPS * STEPS
 LEAD = 7
 RAW_BUFS = 6
-VECTOR_DIFF_EVERY = 4
+VECTOR_TILES = 6
+SHARED_HEAD_SAMPLES = (1, 3, 5)
 
 
 def tile_ta_block_pa_v_kernel(tc, xm, Wq, bq, Wk, bk, Wr, br, q, k, grad_out, out_0, out_1):
@@ -33,15 +35,13 @@ def tile_ta_block_pa_v_kernel(tc, xm, Wq, bq, Wk, bk, Wr, br, q, k, grad_out, ou
         sb = ctx.enter_context(tc.tile_pool(name="sb", bufs=1))
         ps = ctx.enter_context(tc.psum_pool(name="ps", bufs=1))
         ctx.enter_context(tc.manual_schedule())
-        ctx.enter_context(nc.allow_low_precision(reason="the sums are float32; their store is dz1's one rounding to bfloat16"))
+        ctx.enter_context(nc.allow_low_precision(reason="float32 sums whose store is dz1's one rounding to bfloat16"))
 
         def sbuf(tag, width, dtype, bufs=1):
             return sb.tile([P, width], dtype, tag=tag, name=tag, bufs=bufs, align_bytes=64)
 
-        bank_bufs = {"diff": 2, "dd": 2, "dq": 2, "dk": 2}
-
         def bank(tag):
-            return ps.tile([P, BANK], F32, tag=tag, name=tag, bufs=bank_bufs[tag])
+            return ps.tile([P, BANK], F32, tag=tag, name=tag, bufs=2)
 
         def copy(engine, out, in_):
             if engine == "scalar":
@@ -49,17 +49,29 @@ def tile_ta_block_pa_v_kernel(tc, xm, Wq, bq, Wk, bk, Wr, br, q, k, grad_out, ou
             else:
                 nc.vector.tensor_copy(out=out, in_=in_)
 
-        def quantize(fmt, codes, scales, first, values):
-            cols = slice(first, first + values.shape[1] // 4)
+        def quantize(fmt, codes, scales, first_word, values):
+            cols = slice(first_word, first_word + values.shape[1] // 4)
             nc.vector.quantize_mx(out=codes[:, cols].bitcast(fmt), scales=scales[:, cols], in_=values)
 
-        sources = [Wr[512 * s : 512 * (s + 1), :].rearrange("(p j) h -> p j h", j=4) for s in range(2)]
+        def multiply_mx(out, left, left_cols, right, right_cols, start, stop):
+            (left_codes, left_scales, left_fmt), (right_codes, right_scales, right_fmt) = left, right
+            nc.tensor.matmul_mx(
+                out=out,
+                lhsT=left_codes[:, left_cols].bitcast(left_fmt),
+                lhsT_scale=left_scales[:, left_cols],
+                rhs=right_codes[:, right_cols].bitcast(right_fmt),
+                rhs_scale=right_scales[:, right_cols],
+                start=start,
+                stop=stop,
+            )
+
+        sources = [Wr[BANK * s : BANK * (s + 1), :].rearrange("(p a j) h -> p a (j h)", a=1, j=4) for s in range(2)]
         sources.extend(grad_out[n].rearrange("(s p j) g t -> p s (j g t)", s=2, j=4) for n in range(N))
-        for w in (Wq, Wk):
-            rows = w.rearrange("(p j) c -> p j c", j=4)
+        for weight in (Wq, Wk):
+            rows = weight.rearrange("(p j) c -> p j c", j=4)
             sources.extend(rows[:, :, 512 * half : 512 * (half + 1)] for half in range(2))
         sources.extend(xm[16 * half : 16 * (half + 1)].rearrange("n (m c) f -> m n (c f)", c=8) for half in range(2))
-        WR_RAW, GO_RAW, W1_RAW, XM_RAW = 0, 2, 2 + N, 6 + N
+        wr_first, go_first, w1_first, xm_first = 0, 2, 2 + N, 6 + N
         raw = []
 
         def load_next():
@@ -72,7 +84,7 @@ def tile_ta_block_pa_v_kernel(tc, xm, Wq, bq, Wk, bk, Wr, br, q, k, grad_out, ou
         q_raw, k_raw = {}, {}
 
         def load_saved(grp):
-            for name, src, tiles, bufs in (("k_raw", k, k_raw, 1), ("q_raw", q, q_raw, 2)):
+            for name, src, tiles, bufs in (("q_raw", q, q_raw, 2), ("k_raw", k, k_raw, 1)):
                 tiles[grp] = sbuf(name, 512, F32, bufs)
                 nc.sync.dma_start(
                     out=tiles[grp][:].rearrange("p (n w) -> p n w", n=GROUP),
@@ -80,153 +92,146 @@ def tile_ta_block_pa_v_kernel(tc, xm, Wq, bq, Wk, bk, Wr, br, q, k, grad_out, ou
                 )
 
         load_saved(0)
-        for first_loads in range(RAW_BUFS):
+        for slot in range(RAW_BUFS):
             load_next()
 
         ident = sbuf("ident", P, F32)
         make_identity(nc, ident[:])
-        warm = sbuf("warm", 16, F32)
-        nc.vector.memset(warm[:, 0:8], 0.0)
-        nc.scalar.activation(out=warm[:, 8:16], in_=warm[:, 0:8], func=ACT.Tanh)
 
-        wr_codes, wr_scales = sbuf("wr_codes", 1024, U32), sbuf("wr_scales", 1024, U8)
-        w1_codes, w1_scales = sbuf("w1_codes", 2048, U32), sbuf("w1_scales", 2048, U8)
-        xm_codes, xm_scales = sbuf("xm_codes", 1024, U32), sbuf("xm_scales", 1024, U8)
-        dz_codes, dz_scales = sbuf("dz_codes", 1024, U32), sbuf("dz_scales", 1024, U8)
-        dqt_codes, dqt_scales = sbuf("dqt_codes", 512, U32), sbuf("dqt_scales", 512, U8)
+        wr_mx = sbuf("wr_codes", 1024, U32), sbuf("wr_scales", 1024, U8), E4M3
+        w1_mx = sbuf("w1_codes", 2048, U32), sbuf("w1_scales", 2048, U8), E4M3
+        xm_mx = sbuf("xm_codes", 1024, U32), sbuf("xm_scales", 1024, U8), E4M3
+        dz_mx = sbuf("dz_codes", 1024, U32), sbuf("dz_scales", 1024, U8), E5M2
+        dq_mx = sbuf("dq_codes", 512, U32), sbuf("dq_scales", 512, U8), E5M2
         for s in range(2):
             last_group = slice(BANK * (s + 1) - P, BANK * (s + 1))
-            nc.gpsimd.memset(dz_codes[:, last_group], 0)
-            nc.gpsimd.memset(dz_scales[:, last_group], 0)
+            nc.gpsimd.memset(dz_mx[0][:, last_group], 0)
+            nc.gpsimd.memset(dz_mx[1][:, last_group], 0)
         dq_pairs = sbuf("dq_pairs", 2048, BF16)
         dq_tokens = sbuf("dq_tokens", 2048, BF16)
 
-        k_wide, q_wide, squares, woven, go_codes, go_scales, dp_neg, dq_sums, dk_sums, dz = ({} for d in range(10))
-
-        def spread(step):
-            grp, gq = divmod(step, STEPS)
-            if gq == 0:
-                k_wide[grp] = sbuf("k_wide", 2 * BANK, F32, 2)
-                for tq in range(2):
-                    src = k_raw[grp][:].rearrange("p (n h a o t) -> p a h o n t", h=4, a=2, o=1, t=8)[:, tq]
-                    nc.vector.tensor_copy(
-                        out=k_wide[grp][:, BANK * tq : BANK * (tq + 1)].rearrange("p (h g n t) -> p h g n t", h=4, g=2, t=8),
-                        in_=src.to_broadcast([P, 4, 2, GROUP, 8]),
-                    )
-            src = q_raw[grp][:].rearrange("p (n h g s) -> p h g n s", h=4, g=2, s=8)[:, :, :, :, gq : gq + 1]
-            src = src.to_broadcast([P, 4, 2, GROUP, 8])
-            q_wide[step] = sbuf("q_wide", 2 * BANK, F32, 2)
-            if step % VECTOR_DIFF_EVERY == VECTOR_DIFF_EVERY - 1:
-                for tq in range(2):
-                    cols = slice(BANK * tq, BANK * (tq + 1))
-                    nc.vector.tensor_tensor(
-                        out=q_wide[step][:, cols].rearrange("p (h g n t) -> p h g n t", h=4, g=2, t=8),
-                        in0=k_wide[grp][:, cols].rearrange("p (h g n t) -> p h g n t", h=4, g=2, t=8),
-                        in1=src,
-                        op=ALU.subtract,
-                    )
-            else:
-                nc.vector.tensor_scalar(
-                    out=q_wide[step][:, 0:BANK].rearrange("p (h g n t) -> p h g n t", h=4, g=2, t=8),
-                    in0=src,
-                    scalar1=-1.0,
-                    scalar2=None,
-                    op0=ALU.mult,
-                )
+        k_wide, to_turn, squares, woven, go_mx, dp_neg, dq_sums, dk_sums, dz, staged = ({} for name in range(10))
 
         def add_turned(out, block, start, stop):
             nc.tensor.matmul(out, lhsT=block, rhs=ident[:], start=start, stop=stop, is_transpose=True)
 
-        def differences(step):
+        def widen_k(grp):
+            k_wide[grp] = sbuf("k_wide", 2 * BANK, F32, 2)
+            for tq in range(2):
+                src = k_raw[grp][:].rearrange("p (n h b o e) -> p b h o n e", h=4, b=2, o=1, e=8)[:, tq]
+                nc.vector.tensor_copy(
+                    out=k_wide[grp][:, BANK * tq : BANK * (tq + 1)].rearrange("p (h a n e) -> p h a n e", h=4, a=2, e=8),
+                    in_=src.to_broadcast([P, 4, 2, GROUP, 8]),
+                )
+
+        def prepare_differences(step):
+            grp, gq = divmod(step, STEPS)
+            q_step = q_raw[grp][:].rearrange("p (n h a s) -> p h a n s", h=4, a=2, s=8)[:, :, :, :, gq : gq + 1]
+            if grp == 0:
+                if gq % 2 == 0:
+                    to_turn["shared"] = sbuf("to_turn", 2 * BANK, F32, 3)
+                to_turn[step] = to_turn["shared"][:, BANK * (gq % 2) : BANK * (gq % 2 + 1)]
+                nc.vector.tensor_scalar(
+                    out=to_turn[step].rearrange("p (h a n e) -> p h a n e", h=4, a=2, e=8),
+                    in0=q_step.to_broadcast([P, 4, 2, GROUP, 8]),
+                    scalar1=-1.0,
+                    scalar2=None,
+                    op0=ALU.mult,
+                )
+            else:
+                q_row = sbuf("q_row", 64, F32, 2)
+                nc.vector.tensor_copy(out=q_row[:].rearrange("p (h a n o) -> p h a n o", h=4, a=2, o=1), in_=q_step)
+                to_turn[step] = sbuf("to_turn", 2 * BANK, F32, 3)
+                nc.gpsimd.tensor_tensor(
+                    out=to_turn[step][:].rearrange("p (b x e) -> p b x e", b=2, e=8),
+                    in0=k_wide[grp][:].rearrange("p (b x e) -> p b x e", b=2, e=8),
+                    in1=q_row[:].rearrange("p (b x o) -> p b x o", b=1, o=1).to_broadcast([P, 2, 64, 8]),
+                    op=ALU.subtract,
+                )
+
+        def tanh_of_differences(step):
             grp = step // STEPS
             squares[step] = sbuf("squares", 2 * BANK, F32, LEAD + 1)
-            banks = []
+            diffs = [bank("diff"), bank("diff")]
             for tq in range(2):
-                diff = bank("diff")
                 for h in range(4):
                     cols = slice(P * h, P * (h + 1))
                     tile_cols = slice(BANK * tq + P * h, BANK * tq + P * (h + 1))
-                    if step % VECTOR_DIFF_EVERY == VECTOR_DIFF_EVERY - 1:
-                        add_turned(diff[:, cols], q_wide[step][:, tile_cols], True, True)
+                    if grp == 0:
+                        add_turned(diffs[tq][:, cols], to_turn[step][:, cols], True, False)
+                        add_turned(diffs[tq][:, cols], k_wide[grp][:, tile_cols], False, True)
                     else:
-                        add_turned(diff[:, cols], q_wide[step][:, cols], True, False)
-                        add_turned(diff[:, cols], k_wide[grp][:, tile_cols], False, True)
-                banks.append(diff)
+                        add_turned(diffs[tq][:, cols], to_turn[step][:, tile_cols], True, True)
             for tq in range(2):
-                nc.scalar.activation(out=squares[step][:, BANK * tq : BANK * (tq + 1)], in_=banks[tq][:], func=ACT.Tanh)
+                nc.scalar.activation(out=squares[step][:, BANK * tq : BANK * (tq + 1)], in_=diffs[tq][:], func=ACT.Tanh)
 
         def square(step):
             nc.scalar.activation(out=squares[step][:], in_=squares[step][:], func=ACT.Square)
 
-        def weave(sample, engines):
+        def weave_wr(s):
+            if s == 0:
+                staged["wr"] = sbuf("staged", 4096, BF16, 3)
+            nc.vector.tensor_copy(
+                out=staged["wr"][:].rearrange("p (s h m j) -> p s m h j", s=2, h=4, j=4)[:, s],
+                in_=raw[wr_first + s][:].rearrange("p (j m h) -> p m h j", j=4, h=4),
+            )
+
+        def weave_go(sample, engine, tiles):
             grp, n = divmod(sample, GROUP)
-            if n == 0:
+            if grp not in woven:
                 woven[grp] = sbuf("woven", 16384, BF16, 2)
-            dst = woven[grp][:].rearrange("p (l s g n t j) -> p n s g l t j", s=2, g=2, n=GROUP, t=8, j=4)[:, n]
-            src = raw[GO_RAW + sample][:].rearrange("p (s j g l t) -> p s g l t j", s=2, j=4, g=2, t=8)
-            if engines[0] == engines[1]:
-                copy(engines[0], dst, src)
-            else:
-                for s in range(2):
-                    copy(engines[s], dst[:, s], src[:, s])
-            load_next()
+            copy(
+                engine,
+                woven[grp][:].rearrange("p (l s a n e j) -> p n s a l e j", s=2, a=2, n=GROUP, e=8, j=4)[:, n, :, :, tiles],
+                raw[go_first + sample][:].rearrange("p (s j a l e) -> p s a l e j", s=2, j=4, a=2, e=8)[:, :, :, tiles],
+            )
 
         def quantize_go(step):
-            grp, r = divmod(step, STEPS)
-            go_codes[step], go_scales[step] = sbuf("go_codes", 512, U32, 3), sbuf("go_scales", 512, U8, 3)
-            quantize(E5, go_codes[step], go_scales[step], 0, woven[grp][:, 2048 * r : 2048 * (r + 1)])
+            grp, gq = divmod(step, STEPS)
+            go_mx[step] = sbuf("go_codes", 512, U32, 4), sbuf("go_scales", 512, U8, 4), E5M2
+            quantize(E5M2, go_mx[step][0], go_mx[step][1], 0, woven[grp][:, 2048 * gq : 2048 * (gq + 1)])
 
-        def multiply(step):
-            dd_banks = []
-            for u in range(2):
-                dd = bank("dd")
+        def multiply_dd(step):
+            dd = [bank("dd"), bank("dd")]
+            for tq in range(2):
                 for s in range(2):
-                    cols = slice(P * (2 * u + s), P * (2 * u + s + 1))
-                    w_cols = slice(BANK * s, BANK * (s + 1))
-                    nc.tensor.matmul_mx(
-                        out=dd[:],
-                        lhsT=go_codes[step][:, cols].bitcast(E5),
-                        lhsT_scale=go_scales[step][:, cols],
-                        rhs=wr_codes[:, w_cols].bitcast(E4),
-                        rhs_scale=wr_scales[:, w_cols],
-                        start=(s == 0),
-                        stop=(s == 1),
-                    )
-                dd_banks.append(dd)
-            for u in range(2):
-                dp_neg[step, u] = sbuf("dp_neg", BANK, F32, 4)
+                    pairs = slice(P * (2 * tq + s), P * (2 * tq + s + 1))
+                    multiply_mx(dd[tq][:], go_mx[step], pairs, wr_mx, slice(BANK * s, BANK * (s + 1)), s == 0, s == 1)
+            for tq in range(2):
+                dp_neg[step, tq] = sbuf("dp_neg", BANK, F32, 4)
                 nc.vector.scalar_tensor_tensor(
-                    out=dp_neg[step, u][:],
-                    in0=squares[step][:, BANK * u : BANK * (u + 1)],
+                    out=dp_neg[step, tq][:],
+                    in0=squares[step][:, BANK * tq : BANK * (tq + 1)],
                     scalar=1.0,
-                    in1=dd_banks[u][:],
+                    in1=dd[tq][:],
                     op0=ALU.subtract,
                     op1=ALU.mult,
                 )
 
-        def add_up(step):
-            grp, gq = divmod(step, STEPS)
+        def add_dq(step):
             dq_sums[step] = bank("dq")
+            for tq in range(2):
+                for h in range(4):
+                    cols = slice(P * h, P * (h + 1))
+                    add_turned(dq_sums[step][:, cols], dp_neg[step, tq][:, cols], tq == 0 and h == 0, tq == 1 and h == 3)
+
+        def add_dk(step):
+            grp, gq = divmod(step, STEPS)
             if gq == 0:
                 dk_sums[grp] = [bank("dk"), bank("dk")]
             for tq in range(2):
                 for h in range(4):
                     cols = slice(P * h, P * (h + 1))
-                    add_turned(dq_sums[step][:, cols], dp_neg[step, tq][:, cols], tq == 0 and h == 0, tq == 1 and h == 3)
-            for tq in range(2):
-                for h in range(4):
-                    cols = slice(P * h, P * (h + 1))
-                    add_turned(
-                        dk_sums[grp][tq][:, cols], dp_neg[step, tq][:, cols], gq == 0 and h == 0, gq == STEPS - 1 and h == 3
-                    )
+                    first, final = gq == 0 and h == 0, gq == STEPS - 1 and h == 3
+                    add_turned(dk_sums[grp][tq][:, cols], dp_neg[step, tq][:, cols], first, final)
 
         def round_dq(step):
             grp, gq = divmod(step, STEPS)
             if gq == 0:
-                dz[grp] = sbuf("dz", 1024, BF16, 2)
+                dz[grp] = sbuf("dz", 2 * BANK, BF16, 2)
             nc.vector.tensor_reduce(
-                out=dz[grp][:, 0:BANK].rearrange("p (n g s h) -> p s n g h", g=2, s=8, h=4)[:, gq],
-                in_=dq_sums[step][:].rearrange("p (h g n t) -> p n g h t", h=4, g=2, t=8),
+                out=dz[grp][:, 0:BANK].rearrange("p (n a s h) -> p s n a h", a=2, s=8, h=4)[:, gq],
+                in_=dq_sums[step][:].rearrange("p (h a n e) -> p n a h e", h=4, a=2, e=8),
                 axis=mybir.AxisListType.X,
                 op=ALU.add,
                 negate=True,
@@ -234,65 +239,54 @@ def tile_ta_block_pa_v_kernel(tc, xm, Wq, bq, Wk, bk, Wr, br, q, k, grad_out, ou
 
         def round_dk(grp, tq):
             nc.vector.tensor_reduce(
-                out=dz[grp][:, BANK : 2 * BANK].rearrange("p (n a t h) -> p a n t h", a=2, t=8, h=4)[:, tq],
-                in_=dk_sums[grp][tq][:].rearrange("p (h g n t) -> p n t h g", h=4, g=2, t=8),
+                out=dz[grp][:, BANK : 2 * BANK].rearrange("p (n b e h) -> p b n e h", b=2, e=8, h=4)[:, tq],
+                in_=dk_sums[grp][tq][:].rearrange("p (h a n e) -> p n e h a", h=4, a=2, e=8),
                 axis=mybir.AxisListType.X,
                 op=ALU.add,
             )
 
+        def quantize_dz(grp, s):
+            quantize(E5M2, dz_mx[0], dz_mx[1], BANK * s + P * grp, dz[grp][:, BANK * s : BANK * (s + 1)])
+
         def pair_dq(grp):
             nc.scalar.copy(
-                out=dq_pairs[:].rearrange("p (h u c e) -> p h u c e", h=4, u=2, e=2)[:, :, :, 32 * grp : 32 * (grp + 1), :],
-                in_=dz[grp][:, 0:BANK].rearrange("p (c u e h) -> p h u c e", u=2, e=2, h=4),
+                out=dq_pairs[:].rearrange("p (h u r i) -> p h u r i", h=4, u=2, i=2)[:, :, :, 32 * grp : 32 * (grp + 1), :],
+                in_=dz[grp][:, 0:BANK].rearrange("p (r u i h) -> p h u r i", u=2, i=2, h=4),
             )
 
-        def quantize_dz(grp, s):
-            quantize(E5, dz_codes, dz_scales, BANK * s + P * grp, dz[grp][:, BANK * s : BANK * (s + 1)])
+        def pair_xm(half):
+            if half == 0:
+                staged["xm_pairs"] = sbuf("staged", 4096, BF16, 3)
+            nc.vector.tensor_copy(
+                out=staged["xm_pairs"][:].bitcast(F32).rearrange("p (c u b n f) -> p b c u n f", u=2, b=2, n=16, f=4)[:, half],
+                in_=raw[xm_first + half][:].bitcast(F32).rearrange("p (n c f u) -> p c u n f", c=8, f=4, u=2),
+            )
 
-        def turn_words(engine, dst, src, pair):
+        def turn_words(dst, src, part):
             turned = bank("diff")
             for i in range(4):
-                cols = slice(P * (4 * pair + i), P * (4 * pair + i + 1))
+                cols = slice(P * (4 * part + i), P * (4 * part + i + 1))
                 nc.tensor.transpose(turned[:, P * i : P * (i + 1)], src[:].bitcast(F32)[:, cols], ident[:])
-            copy(
-                engine,
-                dst[:].bitcast(F32)[:, BANK * pair : BANK * (pair + 1)].rearrange("p (c m u) -> p c m u", c=2, u=2),
-                turned[:].rearrange("p (c u m) -> p c m u", c=2, u=2),
+            nc.scalar.copy(
+                out=dst[:].bitcast(F32)[:, BANK * part : BANK * (part + 1)].rearrange("p (c m u) -> p c m u", c=2, u=2),
+                in_=turned[:].rearrange("p (c u m) -> p c m u", c=2, u=2),
             )
-
-        staged = {}
 
         def weave_w1(s, half):
             if half == 0:
                 staged["w1", s] = sbuf("staged", 4096, BF16, 3)
-            for a in range(2):
-                nc.scalar.copy(
-                    out=staged["w1", s][:].rearrange("p (a c f m j) -> p a f m c j", a=2, c=4, f=2, j=4)[:, a, half],
-                    in_=raw[W1_RAW + 2 * s + half][:].rearrange("p (j m a c) -> p a m c j", j=4, a=2, c=4)[:, a],
+            for b, engine in enumerate(("vector", "scalar")):
+                copy(
+                    engine,
+                    staged["w1", s][:].rearrange("p (b c f m j) -> p b f m c j", b=2, c=4, f=2, j=4)[:, b, half],
+                    raw[w1_first + 2 * s + half][:].rearrange("p (j m b c) -> p b m c j", j=4, b=2, c=4)[:, b],
                 )
-
-        def sort_xm(half):
-            if half == 0:
-                staged["xm_words"] = sbuf("staged", 4096, BF16, 3)
-            nc.vector.tensor_copy(
-                out=staged["xm_words"][:].bitcast(F32).rearrange("p (c u a n f) -> p a c u n f", u=2, a=2, n=16, f=4)[:, half],
-                in_=raw[XM_RAW + half][:].bitcast(F32).rearrange("p (n c f u) -> p c u n f", c=8, f=4, u=2),
-            )
 
         def multiply_dx(c, tag, engine, groups):
             acc = bank(tag)
             for s in range(2):
-                cols = slice(1024 * s + P * c, 1024 * s + P * (c + 1))
-                z_cols = slice(BANK * s, BANK * (s + 1))
-                nc.tensor.matmul_mx(
-                    out=acc[:],
-                    lhsT=w1_codes[:, cols].bitcast(E4),
-                    lhsT_scale=w1_scales[:, cols],
-                    rhs=dz_codes[:, z_cols].bitcast(E5),
-                    rhs_scale=dz_scales[:, z_cols],
-                    start=(s == 0),
-                    stop=(s == 1),
-                )
+                channels = slice(1024 * s + P * c, 1024 * s + P * (c + 1))
+                multiply_mx(acc[:], w1_mx, channels, dz_mx, slice(BANK * s, BANK * (s + 1)), s == 0, s == 1)
             samples = slice(GROUP * groups.start, GROUP * groups.stop)
             copy(
                 engine,
@@ -308,20 +302,10 @@ def tile_ta_block_pa_v_kernel(tc, xm, Wq, bq, Wk, bk, Wr, br, q, k, grad_out, ou
 
         def multiply_dwq(h, half, tag, engine):
             acc = bank(tag)
-            cols = slice(P * h, P * (h + 1))
-            x_cols = slice(BANK * half, BANK * (half + 1))
-            nc.tensor.matmul_mx(
-                out=acc[:],
-                lhsT=dqt_codes[:, cols].bitcast(E5),
-                lhsT_scale=dqt_scales[:, cols],
-                rhs=xm_codes[:, x_cols].bitcast(E4),
-                rhs_scale=xm_scales[:, x_cols],
-                start=True,
-                stop=True,
-            )
+            multiply_mx(acc[:], dq_mx, slice(P * h, P * (h + 1)), xm_mx, slice(BANK * half, BANK * (half + 1)), True, True)
             copy(
                 engine,
-                staged["dwq"][:].rearrange("p (h m a c) -> p h a m c", h=4, a=2, c=4)[:, h, half],
+                staged["dwq"][:].rearrange("p (h m b c) -> p h b m c", h=4, b=2, c=4)[:, h, half],
                 acc[:].rearrange("p (c m) -> p m c", c=4),
             )
             if half == 1:
@@ -329,98 +313,119 @@ def tile_ta_block_pa_v_kernel(tc, xm, Wq, bq, Wk, bk, Wr, br, q, k, grad_out, ou
                     out=out_1.rearrange("(m h) c -> m h c", h=4)[:, h, :], in_=staged["dwq"][:, C * h : C * (h + 1)]
                 )
 
-        staged["wr"] = sbuf("staged", 4096, BF16, 3)
-        spread(0)
-        for step in range(LEAD):
-            if step < 2:
-                nc.scalar.copy(
-                    out=staged["wr"][:].rearrange("p (s h m j) -> p s m h j", s=2, h=4, j=4)[:, step],
-                    in_=raw[WR_RAW + step][:].rearrange("p (j m h) -> p m h j", j=4, h=4),
-                )
-                load_next()
-            differences(step)
-            spread(step + 1)
-            weave(step, ("vector", "vector"))
-            if step in (2, 3):
-                s = step - 2
-                quantize(E4, wr_codes, wr_scales, BANK * s, staged["wr"][:, 2048 * s : 2048 * (s + 1)])
-            if step == 1:
+        widen_k(0)
+        for s in range(2):
+            prepare_differences(2 * s)
+            prepare_differences(2 * s + 1)
+            weave_wr(s)
+            load_next()
+        for sample in range(GROUP):
+            if sample < LEAD:
+                tanh_of_differences(sample)
+            if sample in SHARED_HEAD_SAMPLES:
+                weave_go(sample, "scalar", slice(TILES // 2, TILES))
+                weave_go(sample, "vector", slice(0, TILES // 2))
+            else:
+                weave_go(sample, "vector", slice(0, TILES))
+            load_next()
+            if sample < 2:
+                quantize(E4M3, wr_mx[0], wr_mx[1], BANK * sample, staged["wr"][:, 2048 * sample : 2048 * (sample + 1)])
+            if sample < STEPS // 2:
+                prepare_differences(STEPS // 2 + sample)
+            if sample == STEPS // 2:
                 load_saved(1)
-        weave(GROUP - 1, ("vector", "vector"))
-        square(0)
-        quantize_go(0)
-        weave(GROUP, ("scalar", "scalar"))
+        for step in range(2):
+            square(step)
+            quantize_go(step)
+        widen_k(1)
+        prepare_differences(LEAD + 1)
+        weave_go(GROUP, "scalar", slice(0, TILES))
+        load_next()
 
         for step in range(ALL_STEPS):
-            multiply(step)
-            if step > 0:
-                add_up(step - 1)
+            sample = step + GROUP + 1
             ahead = step + LEAD
+            multiply_dd(step)
+            if sample < N:
+                weave_go(sample, "scalar", slice(VECTOR_TILES, TILES))
+            if step > 1:
+                round_dq(step - 2)
+            if step > 0:
+                add_dq(step - 1)
+            if 0 < step < ALL_STEPS - 1:
+                add_dk(step - 1)
+            if step > 0 and step % STEPS == 0:
+                for tq in range(2):
+                    round_dk(step // STEPS - 1, tq)
             if ahead < ALL_STEPS:
-                differences(ahead)
-            if step + 1 < ALL_STEPS:
-                square(step + 1)
-                quantize_go(step + 1)
-            if ahead + 1 < ALL_STEPS:
-                spread(ahead + 1)
-                if (ahead + 1) % STEPS == 1 and (ahead + 1) // STEPS + 1 < GROUPS:
-                    load_saved((ahead + 1) // STEPS + 1)
-            if step > STEPS and step % STEPS == 1:
+                tanh_of_differences(ahead)
+            if step + 2 < ALL_STEPS:
+                square(step + 2)
+            if sample < N:
+                weave_go(sample, "vector", slice(0, VECTOR_TILES))
+                load_next()
+            if step + 2 < ALL_STEPS:
+                quantize_go(step + 2)
+            grp, gq = divmod(ahead + 3, STEPS)
+            if grp < GROUPS and gq == 0:
+                widen_k(grp)
+            if grp + 1 < GROUPS and gq == 2:
+                load_saved(grp + 1)
+            if step > STEPS and step % STEPS == 2:
                 pair_dq(step // STEPS - 1)
                 for s in range(2):
                     quantize_dz(step // STEPS - 1, s)
-            sample = step + GROUP + 1
-            if sample < N:
-                weave(sample, ("vector", "scalar"))
-            if step > 0:
-                round_dq(step - 1)
-                if step % STEPS == 0:
-                    for tq in range(2):
-                        round_dk(step // STEPS - 1, tq)
-            late = step - (N - GROUP - 1)
+            if ahead + 2 < ALL_STEPS:
+                prepare_differences(ahead + 2)
+
+            late = sample - N
             if late in (2, 4):
                 s = late // 2 - 1
-                quantize(E4, w1_codes, w1_scales, 1024 * s, staged["w1", s][:])
+                quantize(E4M3, w1_mx[0], w1_mx[1], 1024 * s, staged["w1", s][:])
             if 0 <= late < 4:
                 weave_w1(late // 2, late % 2)
-            if late in (0, 1):
-                sort_xm(late)
+            if 0 <= late < 2:
+                pair_xm(late)
             if late == 3:
                 staged["xm"] = sbuf("staged", 4096, BF16, 3)
             if late in (3, 4):
-                for pair in range(2):
-                    turn_words("scalar", staged["xm"], staged["xm_words"], 2 * (late - 3) + pair)
-            if late in (5, 6):
-                half = late - 5
-                quantize(E4, xm_codes, xm_scales, BANK * half, staged["xm"][:, 2048 * half : 2048 * (half + 1)])
+                for part in range(2 * (late - 3), 2 * (late - 2)):
+                    turn_words(staged["xm"], staged["xm_pairs"], part)
+            if late in (6, 7):
+                half = late - 6
+                quantize(E4M3, xm_mx[0], xm_mx[1], BANK * half, staged["xm"][:, 2048 * half : 2048 * (half + 1)])
             if late == 5:
                 staged["dx"] = sbuf("woven", 4096, F32, 2)
-            if late >= 5:
-                for c in range(2 * (late - 5), 2 * (late - 4)):
+            if late in (5, 6, 7):
+                for c in range(3 * (late - 5), min(3 * (late - 4), 8)):
                     multiply_dx(c, "diff", "scalar", range(GROUPS - 1))
-        for grp in range(GROUPS - 1):
-            store_dx(grp)
+            if late == 7:
+                for done in range(GROUPS - 1):
+                    store_dx(done)
 
-        add_up(ALL_STEPS - 1)
         last = GROUPS - 1
+        round_dq(ALL_STEPS - 2)
+        add_dq(ALL_STEPS - 1)
+        add_dk(ALL_STEPS - 2)
+        add_dk(ALL_STEPS - 1)
         round_dq(ALL_STEPS - 1)
         pair_dq(last)
         round_dk(last, 0)
         quantize_dz(last, 0)
         round_dk(last, 1)
-        turn_words("scalar", dq_tokens, dq_pairs, 0)
-        turn_words("scalar", dq_tokens, dq_pairs, 1)
+        for part in range(2):
+            turn_words(dq_tokens, dq_pairs, part)
         quantize_dz(last, 1)
-        for pair in range(2):
-            quantize(E5, dqt_codes, dqt_scales, 256 * pair, dq_tokens[:, 1024 * pair : 1024 * (pair + 1)])
+        for part in range(2):
+            quantize(E5M2, dq_mx[0], dq_mx[1], 256 * part, dq_tokens[:, 1024 * part : 1024 * (part + 1)])
 
         staged["dwq"] = sbuf("woven", 4096, F32, 2)
         tags = ("dd", "dd", "dq", "dq", "dk", "dk", "diff", "diff")
         jobs = [("dx", c) for c in range(2)] + [("dwq", i) for i in range(8)] + [("dx", c) for c in range(2, 8)]
         for count, (kind, i) in enumerate(jobs):
-            engine = ("scalar", "vector")[count % 2]
+            tag, engine = tags[count % 8], ("scalar", "vector")[count % 2]
             if kind == "dx":
-                multiply_dx(i, tags[count % 8], engine, range(last, GROUPS))
+                multiply_dx(i, tag, engine, range(last, GROUPS))
             else:
-                multiply_dwq(i // 2, i % 2, tags[count % 8], engine)
+                multiply_dwq(i // 2, i % 2, tag, engine)
         store_dx(last)

@@ -20,13 +20,13 @@ P = 128
 BANK = 512
 GROUP = 8
 GROUPS = N // GROUP
+COUPLES = N // 2
 STEPS = 8
-TILES = 2 * STEPS
 ALL_STEPS = GROUPS * STEPS
-LEAD = 7
-RAW_BUFS = 6
-VECTOR_TILES = 6
-SHARED_HEAD_SAMPLES = (1, 3, 5)
+RAW_BUFS = 8
+PSUM_BANKS = {"dd": 4, "dk": 2, "weave": 1, "turn": 1}
+VECTOR_FRAMES = 10
+EXTRAS = 5
 
 
 def tile_ta_block_pa_v_kernel(tc, xm, Wq, bq, Wk, bk, Wr, br, q, k, grad_out, out_0, out_1):
@@ -40,8 +40,8 @@ def tile_ta_block_pa_v_kernel(tc, xm, Wq, bq, Wk, bk, Wr, br, q, k, grad_out, ou
         def sbuf(tag, width, dtype, bufs=1):
             return sb.tile([P, width], dtype, tag=tag, name=tag, bufs=bufs, align_bytes=64)
 
-        def bank(tag):
-            return ps.tile([P, BANK], F32, tag=tag, name=tag, bufs=2)
+        def bank(tag, dtype=F32, width=BANK):
+            return ps.tile([P, width], dtype, tag=tag, name=tag, bufs=PSUM_BANKS[tag])
 
         def copy(engine, out, in_):
             if engine == "scalar":
@@ -65,21 +65,32 @@ def tile_ta_block_pa_v_kernel(tc, xm, Wq, bq, Wk, bk, Wr, br, q, k, grad_out, ou
                 stop=stop,
             )
 
-        sources = [Wr[BANK * s : BANK * (s + 1), :].rearrange("(p a j) h -> p a (j h)", a=1, j=4) for s in range(2)]
-        sources.extend(grad_out[n].rearrange("(s p j) g t -> p s (j g t)", s=2, j=4) for n in range(N))
-        for weight in (Wq, Wk):
-            rows = weight.rearrange("(p j) c -> p j c", j=4)
-            sources.extend(rows[:, :, 512 * half : 512 * (half + 1)] for half in range(2))
-        sources.extend(xm[16 * half : 16 * (half + 1)].rearrange("n (m c) f -> m n (c f)", c=8) for half in range(2))
-        wr_first, go_first, w1_first, xm_first = 0, 2, 2 + N, 6 + N
-        raw = []
+        sources = {}
+        for s in range(2):
+            sources["wr", s] = Wr[BANK * s : BANK * (s + 1), :].rearrange("(p a j) h -> p a (j h)", a=1, j=4)
+        for n in range(N):
+            sources["go", n] = grad_out[n].rearrange("(s p j) g t -> p s (j g t)", s=2, j=4)
+        for s, weight in enumerate((Wq, Wk)):
+            for half in range(2):
+                sources["w1", 2 * s + half] = weight.rearrange("(p j) c -> p j c", j=4)[:, :, 512 * half : 512 * (half + 1)]
+        for half in range(2):
+            sources["xm", half] = xm[16 * half : 16 * (half + 1)].rearrange("n (m c) f -> m n (c f)", c=8)
+        last_read = {("wr", s): s - ALL_STEPS for s in range(2)}
+        for n in range(N):
+            last_read["go", n] = 2 * (n // 2) - 4
+        for i in range(4):
+            last_read["w1", i] = EXTRAS + i
+        for half in range(2):
+            last_read["xm", half] = EXTRAS + 4 + half
+        order = sorted(sources, key=last_read.get)
+        raw = {}
 
         def load_next():
-            if len(raw) < len(sources):
-                src = sources[len(raw)]
+            if len(raw) < len(order):
+                key = order[len(raw)]
                 dst = sbuf("raw", 2048, BF16, RAW_BUFS)
-                nc.sync.dma_start(out=dst[:].rearrange("p (a b) -> p a b", a=src.shape[1]), in_=src)
-                raw.append(dst)
+                nc.sync.dma_start(out=dst[:].rearrange("p (a b) -> p a b", a=sources[key].shape[1]), in_=sources[key])
+                raw[key] = dst
 
         q_raw, k_raw = {}, {}
 
@@ -97,161 +108,162 @@ def tile_ta_block_pa_v_kernel(tc, xm, Wq, bq, Wk, bk, Wr, br, q, k, grad_out, ou
 
         ident = sbuf("ident", P, F32)
         make_identity(nc, ident[:])
+        ident_bf16 = sbuf("ident_bf16", P, BF16)
+        make_identity(nc, ident_bf16[:])
 
         wr_mx = sbuf("wr_codes", 1024, U32), sbuf("wr_scales", 1024, U8), E4M3
         w1_mx = sbuf("w1_codes", 2048, U32), sbuf("w1_scales", 2048, U8), E4M3
         xm_mx = sbuf("xm_codes", 1024, U32), sbuf("xm_scales", 1024, U8), E4M3
-        dz_mx = sbuf("dz_codes", 1024, U32), sbuf("dz_scales", 1024, U8), E5M2
         dq_mx = sbuf("dq_codes", 512, U32), sbuf("dq_scales", 512, U8), E5M2
-        for s in range(2):
-            last_group = slice(BANK * (s + 1) - P, BANK * (s + 1))
-            nc.gpsimd.memset(dz_mx[0][:, last_group], 0)
-            nc.gpsimd.memset(dz_mx[1][:, last_group], 0)
         dq_pairs = sbuf("dq_pairs", 2048, BF16)
         dq_tokens = sbuf("dq_tokens", 2048, BF16)
 
-        k_wide, to_turn, squares, woven, go_mx, dp_neg, dq_sums, dk_sums, dz, staged = ({} for name in range(10))
+        k_sorted, dd_banks, squares, woven, go_mx, dp_neg, dk_sums, dk_tokens, dz, dz_mx, staged = ({} for name in range(11))
 
-        def add_turned(out, block, start, stop):
-            nc.tensor.matmul(out, lhsT=block, rhs=ident[:], start=start, stop=stop, is_transpose=True)
+        def place(step):
+            return 2 * (step // 4) + step % 2, 2 * (step // 2 % 2)
 
-        def widen_k(grp):
-            k_wide[grp] = sbuf("k_wide", 2 * BANK, F32, 2)
-            for tq in range(2):
-                src = k_raw[grp][:].rearrange("p (n h b o e) -> p b h o n e", h=4, b=2, o=1, e=8)[:, tq]
-                nc.vector.tensor_copy(
-                    out=k_wide[grp][:, BANK * tq : BANK * (tq + 1)].rearrange("p (h a n e) -> p h a n e", h=4, a=2, e=8),
-                    in_=src.to_broadcast([P, 4, 2, GROUP, 8]),
-                )
+        def sort_k(grp):
+            k_sorted[grp] = sbuf("k_sorted", 512, F32, 2)
+            nc.vector.tensor_copy(
+                out=k_sorted[grp][:].rearrange("p (c h n t) -> p c h n t", c=4, h=4, n=2),
+                in_=k_raw[grp][:].rearrange("p (c n h t) -> p c h n t", c=4, n=2, h=4),
+            )
 
-        def prepare_differences(step):
-            grp, gq = divmod(step, STEPS)
-            q_step = q_raw[grp][:].rearrange("p (n h a s) -> p h a n s", h=4, a=2, s=8)[:, :, :, :, gq : gq + 1]
-            if grp == 0:
-                if gq % 2 == 0:
-                    to_turn["shared"] = sbuf("to_turn", 2 * BANK, F32, 3)
-                to_turn[step] = to_turn["shared"][:, BANK * (gq % 2) : BANK * (gq % 2 + 1)]
-                nc.vector.tensor_scalar(
-                    out=to_turn[step].rearrange("p (h a n e) -> p h a n e", h=4, a=2, e=8),
-                    in0=q_step.to_broadcast([P, 4, 2, GROUP, 8]),
-                    scalar1=-1.0,
-                    scalar2=None,
-                    op0=ALU.mult,
-                )
-            else:
-                q_row = sbuf("q_row", 64, F32, 2)
-                nc.vector.tensor_copy(out=q_row[:].rearrange("p (h a n o) -> p h a n o", h=4, a=2, o=1), in_=q_step)
-                to_turn[step] = sbuf("to_turn", 2 * BANK, F32, 3)
-                nc.gpsimd.tensor_tensor(
-                    out=to_turn[step][:].rearrange("p (b x e) -> p b x e", b=2, e=8),
-                    in0=k_wide[grp][:].rearrange("p (b x e) -> p b x e", b=2, e=8),
-                    in1=q_row[:].rearrange("p (b x o) -> p b x o", b=1, o=1).to_broadcast([P, 2, 64, 8]),
-                    op=ALU.subtract,
-                )
+        def subtract(step, engine):
+            couple, h = place(step)
+            grp, couple = divmod(couple, 4)
+            blocks = slice(h, h + 2)
+            q_row = sbuf("q_row", 64, F32, 2)
+            nc.vector.tensor_copy(
+                out=q_row[:].rearrange("p (h g n) -> p h g n", h=2, n=2),
+                in_=q_raw[grp][:].rearrange("p (c n h g) -> p c h g n", c=4, n=2, h=4)[:, couple, blocks],
+            )
+            k_row = k_sorted[grp][:].rearrange("p (c h o n t) -> p c h o n t", c=4, h=4, o=1, n=2)[:, couple, blocks]
+            squares[step] = sbuf("squares", 2 * BANK, F32, 6)
+            engine.tensor_tensor(
+                out=squares[step][:].rearrange("p (h g n t) -> p h g n t", h=2, g=T, n=2),
+                in0=k_row.to_broadcast([P, 2, T, 2, T]),
+                in1=q_row[:].rearrange("p (h g n o) -> p h g n o", h=2, n=2, o=1).to_broadcast([P, 2, T, 2, T]),
+                op=ALU.subtract,
+            )
 
-        def tanh_of_differences(step):
-            grp = step // STEPS
-            squares[step] = sbuf("squares", 2 * BANK, F32, LEAD + 1)
-            diffs = [bank("diff"), bank("diff")]
-            for tq in range(2):
-                for h in range(4):
-                    cols = slice(P * h, P * (h + 1))
-                    tile_cols = slice(BANK * tq + P * h, BANK * tq + P * (h + 1))
-                    if grp == 0:
-                        add_turned(diffs[tq][:, cols], to_turn[step][:, cols], True, False)
-                        add_turned(diffs[tq][:, cols], k_wide[grp][:, tile_cols], False, True)
-                    else:
-                        add_turned(diffs[tq][:, cols], to_turn[step][:, tile_cols], True, True)
-            for tq in range(2):
-                nc.scalar.activation(out=squares[step][:, BANK * tq : BANK * (tq + 1)], in_=diffs[tq][:], func=ACT.Tanh)
-
-        def square(step):
-            nc.scalar.activation(out=squares[step][:], in_=squares[step][:], func=ACT.Square)
+        def activate(step, func):
+            nc.scalar.activation(out=squares[step][:], in_=squares[step][:], func=func)
 
         def weave_wr(s):
             if s == 0:
                 staged["wr"] = sbuf("staged", 4096, BF16, 3)
-            nc.vector.tensor_copy(
+            nc.scalar.copy(
                 out=staged["wr"][:].rearrange("p (s h m j) -> p s m h j", s=2, h=4, j=4)[:, s],
-                in_=raw[wr_first + s][:].rearrange("p (j m h) -> p m h j", j=4, h=4),
+                in_=raw["wr", s][:].rearrange("p (j m h) -> p m h j", j=4, h=4),
             )
 
-        def weave_go(sample, engine, tiles):
-            grp, n = divmod(sample, GROUP)
-            if grp not in woven:
-                woven[grp] = sbuf("woven", 16384, BF16, 2)
+        def woven_rows(couple, n, s):
+            if couple not in woven:
+                woven[couple] = sbuf("woven", 4096, BF16, 3)
+            dst = woven[couple][:].rearrange("p (s g n t j) -> p s n g t j", s=2, g=T, n=2, j=4)[:, s, n]
+            src = raw["go", 2 * couple + n][:].rearrange("p (s j g t) -> p s g t j", s=2, j=4, g=T)[:, s]
+            return dst, src
+
+        def weave_go(couple, n, s, engine, frames):
+            dst, src = woven_rows(couple, n, s)
             copy(
                 engine,
-                woven[grp][:].rearrange("p (l s a n e j) -> p n s a l e j", s=2, a=2, n=GROUP, e=8, j=4)[:, n, :, :, tiles],
-                raw[go_first + sample][:].rearrange("p (s j a l e) -> p s a l e j", s=2, j=4, a=2, e=8)[:, :, :, tiles],
+                dst[:, frames].rearrange("p g (a e) j -> p g a j e", e=4),
+                src[:, frames].rearrange("p g (a e) j -> p g a j e", e=4),
             )
 
-        def quantize_go(step):
-            grp, gq = divmod(step, STEPS)
-            go_mx[step] = sbuf("go_codes", 512, U32, 4), sbuf("go_scales", 512, U8, 4), E5M2
-            quantize(E5M2, go_mx[step][0], go_mx[step][1], 0, woven[grp][:, 2048 * gq : 2048 * (gq + 1)])
+        def weave_go_by_matmul(couple, s):
+            dst, src = woven_rows(couple, 0, s)
+            moved = bank("weave", BF16, 2 * BANK)
+            for half in range(2):
+                nc.tensor.matmul(
+                    moved[:, BANK * half : BANK * (half + 1)].rearrange("p (g t j) -> p g t j", g=8, j=4),
+                    lhsT=ident_bf16[:],
+                    rhs=src[:, 8 * half : 8 * (half + 1)],
+                    start=True,
+                    stop=True,
+                )
+            return dst, moved[:].rearrange("p (g t j) -> p g t j", g=T, j=4)
+
+        def quantize_go(couple, s):
+            if s == 0:
+                go_mx[couple] = sbuf("go_codes", 1024, U32, 5), sbuf("go_scales", 1024, U8, 5), E5M2
+            quantize(E5M2, go_mx[couple][0], go_mx[couple][1], BANK * s, woven[couple][:, 2048 * s : 2048 * (s + 1)])
 
         def multiply_dd(step):
+            couple, h = place(step)
             dd = [bank("dd"), bank("dd")]
-            for tq in range(2):
+            for u in range(2):
                 for s in range(2):
-                    pairs = slice(P * (2 * tq + s), P * (2 * tq + s + 1))
-                    multiply_mx(dd[tq][:], go_mx[step], pairs, wr_mx, slice(BANK * s, BANK * (s + 1)), s == 0, s == 1)
-            for tq in range(2):
-                dp_neg[step, tq] = sbuf("dp_neg", BANK, F32, 4)
+                    first = BANK * s + P * (h + u)
+                    pairs = slice(BANK * s, BANK * (s + 1))
+                    multiply_mx(dd[u][:], wr_mx, slice(first, first + P), go_mx[couple], pairs, s == 0, s == 1)
+            dd_banks[step] = dd
+
+        def scale_dd(step):
+            grp, r = divmod(step, STEPS)
+            couple, h = place(step)
+            if r in (0, 2):
+                dp_neg[grp, h] = sbuf("dp_neg", 4096, F32, 3)
+            for u in range(2):
                 nc.vector.scalar_tensor_tensor(
-                    out=dp_neg[step, tq][:],
-                    in0=squares[step][:, BANK * tq : BANK * (tq + 1)],
+                    out=dp_neg[grp, h][:].rearrange("p (u g c x) -> p u c g x", u=2, g=T, c=4)[:, u, couple % 4],
+                    in0=squares[step][:, BANK * u : BANK * (u + 1)].rearrange("p (g x) -> p g x", g=T),
                     scalar=1.0,
-                    in1=dd[tq][:],
+                    in1=dd_banks[step][u][:].rearrange("p (g x) -> p g x", g=T),
                     op0=ALU.subtract,
                     op1=ALU.mult,
                 )
 
-        def add_dq(step):
-            dq_sums[step] = bank("dq")
-            for tq in range(2):
-                for h in range(4):
-                    cols = slice(P * h, P * (h + 1))
-                    add_turned(dq_sums[step][:, cols], dp_neg[step, tq][:, cols], tq == 0 and h == 0, tq == 1 and h == 3)
-
-        def add_dk(step):
-            grp, gq = divmod(step, STEPS)
-            if gq == 0:
-                dk_sums[grp] = [bank("dk"), bank("dk")]
-            for tq in range(2):
-                for h in range(4):
-                    cols = slice(P * h, P * (h + 1))
-                    first, final = gq == 0 and h == 0, gq == STEPS - 1 and h == 3
-                    add_turned(dk_sums[grp][tq][:, cols], dp_neg[step, tq][:, cols], first, final)
-
         def round_dq(step):
-            grp, gq = divmod(step, STEPS)
-            if gq == 0:
+            grp, r = divmod(step, STEPS)
+            couple, h = place(step)
+            blocks = slice(h, h + 2)
+            if r == 0:
                 dz[grp] = sbuf("dz", 2 * BANK, BF16, 2)
             nc.vector.tensor_reduce(
-                out=dz[grp][:, 0:BANK].rearrange("p (n a s h) -> p s n a h", a=2, s=8, h=4)[:, gq],
-                in_=dq_sums[step][:].rearrange("p (h a n e) -> p n a h e", h=4, a=2, e=8),
+                out=dz[grp][:, 0:BANK].rearrange("p (c n g h) -> p c n g h", c=4, n=2, h=4)[:, couple % 4, :, :, blocks],
+                in_=dp_neg[grp, h][:].rearrange("p (u g c n t) -> p c n g u t", u=2, g=T, c=4, n=2)[:, couple % 4],
                 axis=mybir.AxisListType.X,
                 op=ALU.add,
                 negate=True,
             )
 
-        def round_dk(grp, tq):
-            nc.vector.tensor_reduce(
-                out=dz[grp][:, BANK : 2 * BANK].rearrange("p (n b e h) -> p b n e h", b=2, e=8, h=4)[:, tq],
-                in_=dk_sums[grp][tq][:].rearrange("p (h a n e) -> p n e h a", h=4, a=2, e=8),
-                axis=mybir.AxisListType.X,
-                op=ALU.add,
-            )
+        def add_dk(grp, h):
+            if h % 2 == 0:
+                dk_sums[grp, h // 2] = bank("dk", F32, 2 * P)
+            for g in range(T):
+                nc.tensor.matmul(
+                    dk_sums[grp, h // 2][:, P * (h % 2) : P * (h % 2 + 1)],
+                    lhsT=dp_neg[grp, h - h % 2][:, P * (T * (h % 2) + g) : P * (T * (h % 2) + g + 1)],
+                    rhs=ident[:],
+                    start=(h % 2 == 0 and g == 0),
+                    stop=(h % 2 == 1 and g == T - 1),
+                    is_transpose=True,
+                )
+
+        def fetch_dk(grp, half):
+            dk_tokens[grp, half] = sbuf("dk_tokens", 2 * P, F32, 2)
+            nc.scalar.copy(out=dk_tokens[grp, half][:], in_=dk_sums[grp, half][:])
+
+        def turn_dk(grp, half):
+            turned = bank("turn", F32, 2 * P)
+            for i in range(2):
+                nc.tensor.transpose(turned[:, P * i : P * (i + 1)], dk_tokens[grp, half][:, P * i : P * (i + 1)], ident[:])
+            dst = dz[grp][:, BANK : 2 * BANK].rearrange("p (r h) -> p r h", h=4)[:, :, 2 * half : 2 * half + 2]
+            return dst, turned[:].rearrange("p (h r) -> p r h", h=2)
 
         def quantize_dz(grp, s):
-            quantize(E5M2, dz_mx[0], dz_mx[1], BANK * s + P * grp, dz[grp][:, BANK * s : BANK * (s + 1)])
+            if s == 0:
+                dz_mx[grp] = sbuf("dz_codes", 2 * P, U32, 2), sbuf("dz_scales", 2 * P, U8, 2), E5M2
+            quantize(E5M2, dz_mx[grp][0], dz_mx[grp][1], P * s, dz[grp][:, BANK * s : BANK * (s + 1)])
 
-        def pair_dq(grp):
+        def pair_dq(grp, blocks):
             nc.scalar.copy(
-                out=dq_pairs[:].rearrange("p (h u r i) -> p h u r i", h=4, u=2, i=2)[:, :, :, 32 * grp : 32 * (grp + 1), :],
-                in_=dz[grp][:, 0:BANK].rearrange("p (r u i h) -> p h u r i", u=2, i=2, h=4),
+                out=dq_pairs[:].rearrange("p (h u r i) -> p h u r i", h=4, u=2, i=2)[:, blocks, :, 32 * grp : 32 * (grp + 1)],
+                in_=dz[grp][:, 0:BANK].rearrange("p (r u i h) -> p h u r i", u=2, i=2, h=4)[:, blocks],
             )
 
         def pair_xm(half):
@@ -259,18 +271,16 @@ def tile_ta_block_pa_v_kernel(tc, xm, Wq, bq, Wk, bk, Wr, br, q, k, grad_out, ou
                 staged["xm_pairs"] = sbuf("staged", 4096, BF16, 3)
             nc.vector.tensor_copy(
                 out=staged["xm_pairs"][:].bitcast(F32).rearrange("p (c u b n f) -> p b c u n f", u=2, b=2, n=16, f=4)[:, half],
-                in_=raw[xm_first + half][:].bitcast(F32).rearrange("p (n c f u) -> p c u n f", c=8, f=4, u=2),
+                in_=raw["xm", half][:].bitcast(F32).rearrange("p (n c f u) -> p c u n f", c=8, f=4, u=2),
             )
 
-        def turn_words(dst, src, part):
-            turned = bank("diff")
+        def turn_words(dst, src, part, tag):
+            turned = bank(tag)
             for i in range(4):
                 cols = slice(P * (4 * part + i), P * (4 * part + i + 1))
                 nc.tensor.transpose(turned[:, P * i : P * (i + 1)], src[:].bitcast(F32)[:, cols], ident[:])
-            nc.scalar.copy(
-                out=dst[:].bitcast(F32)[:, BANK * part : BANK * (part + 1)].rearrange("p (c m u) -> p c m u", c=2, u=2),
-                in_=turned[:].rearrange("p (c u m) -> p c m u", c=2, u=2),
-            )
+            words = dst[:].bitcast(F32)[:, BANK * part : BANK * (part + 1)]
+            return words.rearrange("p (c m u) -> p c m u", c=2, u=2), turned[:].rearrange("p (c u m) -> p c m u", c=2, u=2)
 
         def weave_w1(s, half):
             if half == 0:
@@ -279,153 +289,171 @@ def tile_ta_block_pa_v_kernel(tc, xm, Wq, bq, Wk, bk, Wr, br, q, k, grad_out, ou
                 copy(
                     engine,
                     staged["w1", s][:].rearrange("p (b c f m j) -> p b f m c j", b=2, c=4, f=2, j=4)[:, b, half],
-                    raw[w1_first + 2 * s + half][:].rearrange("p (j m b c) -> p b m c j", j=4, b=2, c=4)[:, b],
+                    raw["w1", 2 * s + half][:].rearrange("p (j m b c) -> p b m c j", j=4, b=2, c=4)[:, b],
                 )
 
-        def multiply_dx(c, tag, engine, groups):
+        def multiply_dx(grp, half, tag):
+            if half == 0:
+                staged["dx_tokens"] = sbuf("dx_tokens", C, F32)
             acc = bank(tag)
             for s in range(2):
-                channels = slice(1024 * s + P * c, 1024 * s + P * (c + 1))
-                multiply_mx(acc[:], w1_mx, channels, dz_mx, slice(BANK * s, BANK * (s + 1)), s == 0, s == 1)
-            samples = slice(GROUP * groups.start, GROUP * groups.stop)
-            copy(
-                engine,
-                staged["dx"][:].rearrange("p (n c f) -> p c n f", c=8, f=T)[:, c, samples],
-                acc[:].rearrange("p (n f) -> p n f", f=T)[:, samples],
-            )
+                channels = slice(C * s + BANK * half, C * s + BANK * (half + 1))
+                multiply_mx(acc[:], dz_mx[grp], slice(P * s, P * (s + 1)), w1_mx, channels, s == 0, s == 1)
+            return staged["dx_tokens"][:, BANK * half : BANK * (half + 1)], acc[:]
+
+        def turn_dx(half, tag):
+            if half == 0:
+                staged["dx"] = sbuf("dx", C, F32)
+            turned = bank(tag)
+            for c in range(4):
+                first = BANK * half + P * c
+                nc.tensor.transpose(turned[:, P * c : P * (c + 1)], staged["dx_tokens"][:, first : first + P], ident[:])
+            dst = staged["dx"][:].rearrange("p (n b c f) -> p b n c f", b=2, c=4, f=T)[:, half]
+            return dst, turned[:].rearrange("p (c n f) -> p n c f", c=4, f=T)
 
         def store_dx(grp):
             nc.sync.dma_start(
                 out=out_0[GROUP * grp : GROUP * (grp + 1)].rearrange("n (m c) f -> m n (c f)", c=8),
-                in_=staged["dx"][:, 1024 * grp : 1024 * (grp + 1)].rearrange("p (n w) -> p n w", n=GROUP),
+                in_=staged["dx"][:].rearrange("p (n w) -> p n w", n=GROUP),
             )
 
-        def multiply_dwq(h, half, tag, engine):
-            acc = bank(tag)
-            multiply_mx(acc[:], dq_mx, slice(P * h, P * (h + 1)), xm_mx, slice(BANK * half, BANK * (half + 1)), True, True)
-            copy(
-                engine,
-                staged["dwq"][:].rearrange("p (h m b c) -> p h b m c", h=4, b=2, c=4)[:, h, half],
-                acc[:].rearrange("p (c m) -> p m c", c=4),
-            )
-            if half == 1:
-                nc.sync.dma_start(
-                    out=out_1.rearrange("(m h) c -> m h c", h=4)[:, h, :], in_=staged["dwq"][:, C * h : C * (h + 1)]
-                )
-
-        widen_k(0)
-        for s in range(2):
-            prepare_differences(2 * s)
-            prepare_differences(2 * s + 1)
-            weave_wr(s)
-            load_next()
-        for sample in range(GROUP):
-            if sample < LEAD:
-                tanh_of_differences(sample)
-            if sample in SHARED_HEAD_SAMPLES:
-                weave_go(sample, "scalar", slice(TILES // 2, TILES))
-                weave_go(sample, "vector", slice(0, TILES // 2))
-            else:
-                weave_go(sample, "vector", slice(0, TILES))
-            load_next()
-            if sample < 2:
-                quantize(E4M3, wr_mx[0], wr_mx[1], BANK * sample, staged["wr"][:, 2048 * sample : 2048 * (sample + 1)])
-            if sample < STEPS // 2:
-                prepare_differences(STEPS // 2 + sample)
-            if sample == STEPS // 2:
-                load_saved(1)
-        for step in range(2):
-            square(step)
-            quantize_go(step)
-        widen_k(1)
-        prepare_differences(LEAD + 1)
-        weave_go(GROUP, "scalar", slice(0, TILES))
-        load_next()
-
-        for step in range(ALL_STEPS):
-            sample = step + GROUP + 1
-            ahead = step + LEAD
-            multiply_dd(step)
-            if sample < N:
-                weave_go(sample, "scalar", slice(VECTOR_TILES, TILES))
-            if step > 1:
-                round_dq(step - 2)
-            if step > 0:
-                add_dq(step - 1)
-            if 0 < step < ALL_STEPS - 1:
-                add_dk(step - 1)
-            if step > 0 and step % STEPS == 0:
-                for tq in range(2):
-                    round_dk(step // STEPS - 1, tq)
-            if ahead < ALL_STEPS:
-                tanh_of_differences(ahead)
-            if step + 2 < ALL_STEPS:
-                square(step + 2)
-            if sample < N:
-                weave_go(sample, "vector", slice(0, VECTOR_TILES))
-                load_next()
-            if step + 2 < ALL_STEPS:
-                quantize_go(step + 2)
-            grp, gq = divmod(ahead + 3, STEPS)
-            if grp < GROUPS and gq == 0:
-                widen_k(grp)
-            if grp + 1 < GROUPS and gq == 2:
-                load_saved(grp + 1)
-            if step > STEPS and step % STEPS == 2:
-                pair_dq(step // STEPS - 1)
-                for s in range(2):
-                    quantize_dz(step // STEPS - 1, s)
-            if ahead + 2 < ALL_STEPS:
-                prepare_differences(ahead + 2)
-
-            late = sample - N
-            if late in (2, 4):
-                s = late // 2 - 1
-                quantize(E4M3, w1_mx[0], w1_mx[1], 1024 * s, staged["w1", s][:])
-            if 0 <= late < 4:
-                weave_w1(late // 2, late % 2)
-            if 0 <= late < 2:
-                pair_xm(late)
-            if late == 3:
-                staged["xm"] = sbuf("staged", 4096, BF16, 3)
-            if late in (3, 4):
-                for part in range(2 * (late - 3), 2 * (late - 2)):
-                    turn_words(staged["xm"], staged["xm_pairs"], part)
-            if late in (6, 7):
-                half = late - 6
-                quantize(E4M3, xm_mx[0], xm_mx[1], BANK * half, staged["xm"][:, 2048 * half : 2048 * (half + 1)])
-            if late == 5:
-                staged["dx"] = sbuf("woven", 4096, F32, 2)
-            if late in (5, 6, 7):
-                for c in range(3 * (late - 5), min(3 * (late - 4), 8)):
-                    multiply_dx(c, "diff", "scalar", range(GROUPS - 1))
-            if late == 7:
-                for done in range(GROUPS - 1):
-                    store_dx(done)
-
-        last = GROUPS - 1
-        round_dq(ALL_STEPS - 2)
-        add_dq(ALL_STEPS - 1)
-        add_dk(ALL_STEPS - 2)
-        add_dk(ALL_STEPS - 1)
-        round_dq(ALL_STEPS - 1)
-        pair_dq(last)
-        round_dk(last, 0)
-        quantize_dz(last, 0)
-        round_dk(last, 1)
-        for part in range(2):
-            turn_words(dq_tokens, dq_pairs, part)
-        quantize_dz(last, 1)
-        for part in range(2):
+        def quantize_dq(part):
             quantize(E5M2, dq_mx[0], dq_mx[1], 256 * part, dq_tokens[:, 1024 * part : 1024 * (part + 1)])
 
-        staged["dwq"] = sbuf("woven", 4096, F32, 2)
-        tags = ("dd", "dd", "dq", "dq", "dk", "dk", "diff", "diff")
-        jobs = [("dx", c) for c in range(2)] + [("dwq", i) for i in range(8)] + [("dx", c) for c in range(2, 8)]
-        for count, (kind, i) in enumerate(jobs):
-            tag, engine = tags[count % 8], ("scalar", "vector")[count % 2]
-            if kind == "dx":
-                multiply_dx(i, tag, engine, range(last, GROUPS))
-            else:
-                multiply_dwq(i // 2, i % 2, tag, engine)
+        def multiply_dwq(h):
+            if h % 2 == 0:
+                staged["dwq"] = sbuf("staged", 2 * C, F32, 3)
+            rows = staged["dwq"][:, C * (h % 2) : C * (h % 2 + 1)]
+            for half, engine in enumerate(("scalar", "vector")):
+                acc = bank("dd")
+                multiply_mx(acc[:], dq_mx, slice(P * h, P * (h + 1)), xm_mx, slice(BANK * half, BANK * (half + 1)), True, True)
+                copy(
+                    engine,
+                    rows.rearrange("p (m b c) -> p b m c", b=2, c=4)[:, half],
+                    acc[:].rearrange("p (c m) -> p m c", c=4),
+                )
+            nc.sync.dma_start(out=out_1.rearrange("(m h) c -> m h c", h=4)[:, h, :], in_=rows)
+
+        everything, vector_share, scalar_share = slice(0, T), slice(0, VECTOR_FRAMES), slice(VECTOR_FRAMES, T)
+        sort_k(0)
+        for step in range(4):
+            subtract(step, nc.vector)
+        for s in range(2):
+            weave_wr(s)
+            load_next()
+        for n in range(2):
+            for s in range(2):
+                weave_go(0, n, s, "vector", everything)
+            load_next()
+            activate(n, ACT.Tanh)
+        for s in range(2):
+            quantize(E4M3, wr_mx[0], wr_mx[1], BANK * s, staged["wr"][:, 2048 * s : 2048 * (s + 1)])
+            quantize_go(0, s)
+            copy("scalar", *weave_go_by_matmul(1, s))
+            activate(s, ACT.Square)
+        multiply_dd(0)
+        for s in range(2):
+            weave_go(1, 1, s, "vector", everything)
+        for s in range(2):
+            load_next()
+            quantize_go(1, s)
+        activate(2, ACT.Tanh)
+        waiting = [weave_go_by_matmul(2, 0)]
+        weave_go(2, 1, 0, "scalar", everything)
+        load_saved(1)
+
+        last = GROUPS - 1
+        for step in range(ALL_STEPS):
+            grp, r = divmod(step, STEPS)
+            to_weave, s = divmod(step + 5, 2)
+            extra = step - EXTRAS
+            for move in waiting:
+                copy("scalar", *move)
+            waiting.clear()
+            if grp > 0 and r == 5:
+                store_dx(grp - 1)
+            scale_dd(step)
+            if step + 1 < ALL_STEPS:
+                multiply_dd(step + 1)
+            if step > 0:
+                round_dq(step - 1)
+            if grp > 0 and r in (0, 2):
+                fetch_dk(grp - 1, r // 2)
+            if to_weave < COUPLES:
+                weave_go(to_weave, 1, s, "scalar", scalar_share)
+            if step + 2 < ALL_STEPS:
+                activate(step + 2, ACT.Square)
+            if step == ALL_STEPS - 2:
+                pair_dq(last, slice(0, 2))
+            if r >= 6:
+                add_dk(grp, r - 6)
+            if grp > 0 and r < 2:
+                add_dk(grp - 1, r + 2)
+            if grp > 0 and r in (0, 2):
+                waiting.append(turn_dk(grp - 1, r // 2))
+            if step == ALL_STEPS - 2:
+                waiting.append(turn_words(dq_tokens, dq_pairs, 0, "turn"))
+            if step + 3 < ALL_STEPS:
+                activate(step + 3, ACT.Tanh)
+            if step + 4 < 2 * COUPLES:
+                quantize_go((step + 4) // 2, step % 2)
+            if to_weave < COUPLES:
+                weave_go(to_weave, 1, s, "vector", vector_share)
+                waiting.append(weave_go_by_matmul(to_weave, s))
+                if s == 1:
+                    load_next()
+                    load_next()
+            if grp > 0 and r == 1:
+                pair_dq(grp - 1, slice(0, 4))
+            if grp > 0 and r in (1, 3):
+                quantize_dz(grp - 1, r // 2)
+            if r == 2 and grp < last:
+                sort_k(grp + 1)
+            if r == 4 and grp + 1 < last:
+                load_saved(grp + 2)
+            if extra in (3, 5):
+                half = extra // 2 - 1
+                quantize(E4M3, w1_mx[0], w1_mx[1], 1024 * half, staged["w1", half][:])
+            if 0 <= extra < 4:
+                weave_w1(extra // 2, extra % 2)
+                load_next()
+            if extra in (4, 5):
+                pair_xm(extra - 4)
+                load_next()
+            if extra == 7:
+                staged["xm"] = sbuf("staged", 4096, BF16, 3)
+            if 7 <= extra < 11:
+                waiting.append(turn_words(staged["xm"], staged["xm_pairs"], extra - 7, "turn"))
+            if extra in (12, 13):
+                half = extra - 12
+                quantize(E4M3, xm_mx[0], xm_mx[1], BANK * half, staged["xm"][:, 2048 * half : 2048 * (half + 1)])
+            if step == ALL_STEPS - 1:
+                quantize_dq(0)
+            if step + 4 < ALL_STEPS:
+                subtract(step + 4, nc.gpsimd)
+            if grp > 0 and r == 3:
+                waiting.extend(multiply_dx(grp - 1, half, "dk") for half in range(2))
+            if grp > 0 and r == 4:
+                waiting.extend(turn_dx(half, "dk") for half in range(2))
+
+        round_dq(ALL_STEPS - 1)
+        fetch_dk(last, 0)
+        multiply_dwq(0)
+        pair_dq(last, slice(2, 4))
+        add_dk(last, 2)
+        copy("scalar", *turn_dk(last, 0))
+        copy("scalar", *turn_words(dq_tokens, dq_pairs, 1, "weave"))
+        add_dk(last, 3)
+        quantize_dz(last, 0)
+        quantize_dq(1)
+        fetch_dk(last, 1)
+        multiply_dwq(1)
+        copy("scalar", *turn_dk(last, 1))
+        quantize_dz(last, 1)
+        multiply_dwq(2)
+        for half, engine in enumerate(("scalar", "vector")):
+            copy(engine, *multiply_dx(last, half, "dk"))
+        multiply_dwq(3)
+        for half, engine in enumerate(("scalar", "vector")):
+            copy(engine, *turn_dx(half, ("weave", "turn")[half]))
         store_dx(last)

from contextlib import ExitStack

import concourse.mybir as mybir
from concourse.masks import make_identity

N, C, T, H, O = 32, 1024, 16, 512, 1024
FLOPS = 2 * N * T * T * O * H + 2 * N * T * 2 * H * C + 2 * N * T * H * C
BYTES = 2 * (N * C * T + 2 * H * C + O * H + N * O * T * T) + 4 * (2 * N * H * T + N * C * T + H * C)

F32 = mybir.dt.float32
BF16 = mybir.dt.bfloat16
U32 = mybir.dt.uint32
U8 = mybir.dt.uint8
E4M3 = mybir.dt.float8_e4m3fn_x4
E5M2 = mybir.dt.float8_e5m2_x4
ACT = mybir.ActivationFunctionType
ALU = mybir.AluOpType

P = 128
BANK = 512
GROUP = 8
GROUPS = N // GROUP
COUPLES = N // 2
STEPS = 8
ALL_STEPS = GROUPS * STEPS
RAW_BUFS = 8
PSUM_BANKS = {"dd": 4, "dk": 2, "weave": 1, "turn": 1}
VECTOR_FRAMES = 10
EXTRAS = 5


def tile_ta_block_pa_v_kernel(tc, xm, Wq, bq, Wk, bk, Wr, br, q, k, grad_out, out_0, out_1):
    nc = tc.nc
    with ExitStack() as ctx:
        sb = ctx.enter_context(tc.tile_pool(name="sb", bufs=1))
        ps = ctx.enter_context(tc.psum_pool(name="ps", bufs=1))
        ctx.enter_context(tc.manual_schedule())
        ctx.enter_context(nc.allow_low_precision(reason="float32 sums whose store is dz1's one rounding to bfloat16"))

        def sbuf(tag, width, dtype, bufs=1):
            return sb.tile([P, width], dtype, tag=tag, name=tag, bufs=bufs, align_bytes=64)

        def bank(tag, dtype=F32, width=BANK):
            return ps.tile([P, width], dtype, tag=tag, name=tag, bufs=PSUM_BANKS[tag])

        def copy(engine, out, in_):
            if engine == "scalar":
                nc.scalar.copy(out=out, in_=in_)
            else:
                nc.vector.tensor_copy(out=out, in_=in_)

        def quantize(fmt, codes, scales, first_word, values):
            cols = slice(first_word, first_word + values.shape[1] // 4)
            nc.vector.quantize_mx(out=codes[:, cols].bitcast(fmt), scales=scales[:, cols], in_=values)

        def multiply_mx(out, left, left_cols, right, right_cols, start, stop):
            (left_codes, left_scales, left_fmt), (right_codes, right_scales, right_fmt) = left, right
            nc.tensor.matmul_mx(
                out=out,
                lhsT=left_codes[:, left_cols].bitcast(left_fmt),
                lhsT_scale=left_scales[:, left_cols],
                rhs=right_codes[:, right_cols].bitcast(right_fmt),
                rhs_scale=right_scales[:, right_cols],
                start=start,
                stop=stop,
            )

        sources = {}
        for s in range(2):
            sources["wr", s] = Wr[BANK * s : BANK * (s + 1), :].rearrange("(p a j) h -> p a (j h)", a=1, j=4)
        for n in range(N):
            sources["go", n] = grad_out[n].rearrange("(s p j) g t -> p s (j g t)", s=2, j=4)
        for s, weight in enumerate((Wq, Wk)):
            for half in range(2):
                sources["w1", 2 * s + half] = weight.rearrange("(p j) c -> p j c", j=4)[:, :, 512 * half : 512 * (half + 1)]
        for half in range(2):
            sources["xm", half] = xm[16 * half : 16 * (half + 1)].rearrange("n (m c) f -> m n (c f)", c=8)
        last_read = {("wr", s): s - ALL_STEPS for s in range(2)}
        for n in range(N):
            last_read["go", n] = 2 * (n // 2) - 4
        for i in range(4):
            last_read["w1", i] = EXTRAS + i
        for half in range(2):
            last_read["xm", half] = EXTRAS + 4 + half
        order = sorted(sources, key=last_read.get)
        raw = {}

        def load_next():
            if len(raw) < len(order):
                key = order[len(raw)]
                dst = sbuf("raw", 2048, BF16, RAW_BUFS)
                nc.sync.dma_start(out=dst[:].rearrange("p (a b) -> p a b", a=sources[key].shape[1]), in_=sources[key])
                raw[key] = dst

        q_raw, k_raw = {}, {}

        def load_saved(grp):
            for name, src, tiles, bufs in (("q_raw", q, q_raw, 2), ("k_raw", k, k_raw, 1)):
                tiles[grp] = sbuf(name, 512, F32, bufs)
                nc.sync.dma_start(
                    out=tiles[grp][:].rearrange("p (n w) -> p n w", n=GROUP),
                    in_=src[GROUP * grp : GROUP * (grp + 1)].rearrange("n (m h) f -> m n (h f)", h=4),
                )

        load_saved(0)
        for slot in range(RAW_BUFS):
            load_next()

        ident = sbuf("ident", P, F32)
        make_identity(nc, ident[:])
        ident_bf16 = sbuf("ident_bf16", P, BF16)
        make_identity(nc, ident_bf16[:])

        wr_mx = sbuf("wr_codes", 1024, U32), sbuf("wr_scales", 1024, U8), E4M3
        w1_mx = sbuf("w1_codes", 2048, U32), sbuf("w1_scales", 2048, U8), E4M3
        xm_mx = sbuf("xm_codes", 1024, U32), sbuf("xm_scales", 1024, U8), E4M3
        dq_mx = sbuf("dq_codes", 512, U32), sbuf("dq_scales", 512, U8), E5M2
        dq_pairs = sbuf("dq_pairs", 2048, BF16)
        dq_tokens = sbuf("dq_tokens", 2048, BF16)

        k_sorted, dd_banks, squares, woven, go_mx, dp_neg, dk_sums, dk_tokens, dz, dz_mx, staged = ({} for name in range(11))

        def place(step):
            return 2 * (step // 4) + step % 2, 2 * (step // 2 % 2)

        def sort_k(grp):
            k_sorted[grp] = sbuf("k_sorted", 512, F32, 2)
            nc.vector.tensor_copy(
                out=k_sorted[grp][:].rearrange("p (c h n t) -> p c h n t", c=4, h=4, n=2),
                in_=k_raw[grp][:].rearrange("p (c n h t) -> p c h n t", c=4, n=2, h=4),
            )

        def subtract(step, engine):
            couple, h = place(step)
            grp, couple = divmod(couple, 4)
            blocks = slice(h, h + 2)
            q_row = sbuf("q_row", 64, F32, 2)
            nc.vector.tensor_copy(
                out=q_row[:].rearrange("p (h g n) -> p h g n", h=2, n=2),
                in_=q_raw[grp][:].rearrange("p (c n h g) -> p c h g n", c=4, n=2, h=4)[:, couple, blocks],
            )
            k_row = k_sorted[grp][:].rearrange("p (c h o n t) -> p c h o n t", c=4, h=4, o=1, n=2)[:, couple, blocks]
            squares[step] = sbuf("squares", 2 * BANK, F32, 6)
            engine.tensor_tensor(
                out=squares[step][:].rearrange("p (h g n t) -> p h g n t", h=2, g=T, n=2),
                in0=k_row.to_broadcast([P, 2, T, 2, T]),
                in1=q_row[:].rearrange("p (h g n o) -> p h g n o", h=2, n=2, o=1).to_broadcast([P, 2, T, 2, T]),
                op=ALU.subtract,
            )

        def activate(step, func):
            nc.scalar.activation(out=squares[step][:], in_=squares[step][:], func=func)

        def weave_wr(s):
            if s == 0:
                staged["wr"] = sbuf("staged", 4096, BF16, 3)
            nc.scalar.copy(
                out=staged["wr"][:].rearrange("p (s h m j) -> p s m h j", s=2, h=4, j=4)[:, s],
                in_=raw["wr", s][:].rearrange("p (j m h) -> p m h j", j=4, h=4),
            )

        def woven_rows(couple, n, s):
            if couple not in woven:
                woven[couple] = sbuf("woven", 4096, BF16, 3)
            dst = woven[couple][:].rearrange("p (s g n t j) -> p s n g t j", s=2, g=T, n=2, j=4)[:, s, n]
            src = raw["go", 2 * couple + n][:].rearrange("p (s j g t) -> p s g t j", s=2, j=4, g=T)[:, s]
            return dst, src

        def weave_go(couple, n, s, engine, frames):
            dst, src = woven_rows(couple, n, s)
            copy(
                engine,
                dst[:, frames].rearrange("p g (a e) j -> p g a j e", e=4),
                src[:, frames].rearrange("p g (a e) j -> p g a j e", e=4),
            )

        def weave_go_by_matmul(couple, s):
            dst, src = woven_rows(couple, 0, s)
            moved = bank("weave", BF16, 2 * BANK)
            for half in range(2):
                nc.tensor.matmul(
                    moved[:, BANK * half : BANK * (half + 1)].rearrange("p (g t j) -> p g t j", g=8, j=4),
                    lhsT=ident_bf16[:],
                    rhs=src[:, 8 * half : 8 * (half + 1)],
                    start=True,
                    stop=True,
                )
            return dst, moved[:].rearrange("p (g t j) -> p g t j", g=T, j=4)

        def quantize_go(couple, s):
            if s == 0:
                go_mx[couple] = sbuf("go_codes", 1024, U32, 5), sbuf("go_scales", 1024, U8, 5), E5M2
            quantize(E5M2, go_mx[couple][0], go_mx[couple][1], BANK * s, woven[couple][:, 2048 * s : 2048 * (s + 1)])

        def multiply_dd(step):
            couple, h = place(step)
            dd = [bank("dd"), bank("dd")]
            for u in range(2):
                for s in range(2):
                    first = BANK * s + P * (h + u)
                    pairs = slice(BANK * s, BANK * (s + 1))
                    multiply_mx(dd[u][:], wr_mx, slice(first, first + P), go_mx[couple], pairs, s == 0, s == 1)
            dd_banks[step] = dd

        def scale_dd(step):
            grp, r = divmod(step, STEPS)
            couple, h = place(step)
            if r in (0, 2):
                dp_neg[grp, h] = sbuf("dp_neg", 4096, F32, 3)
            for u in range(2):
                nc.vector.scalar_tensor_tensor(
                    out=dp_neg[grp, h][:].rearrange("p (u g c x) -> p u c g x", u=2, g=T, c=4)[:, u, couple % 4],
                    in0=squares[step][:, BANK * u : BANK * (u + 1)].rearrange("p (g x) -> p g x", g=T),
                    scalar=1.0,
                    in1=dd_banks[step][u][:].rearrange("p (g x) -> p g x", g=T),
                    op0=ALU.subtract,
                    op1=ALU.mult,
                )

        def round_dq(step):
            grp, r = divmod(step, STEPS)
            couple, h = place(step)
            blocks = slice(h, h + 2)
            if r == 0:
                dz[grp] = sbuf("dz", 2 * BANK, BF16, 2)
            nc.vector.tensor_reduce(
                out=dz[grp][:, 0:BANK].rearrange("p (c n g h) -> p c n g h", c=4, n=2, h=4)[:, couple % 4, :, :, blocks],
                in_=dp_neg[grp, h][:].rearrange("p (u g c n t) -> p c n g u t", u=2, g=T, c=4, n=2)[:, couple % 4],
                axis=mybir.AxisListType.X,
                op=ALU.add,
                negate=True,
            )

        def add_dk(grp, h):
            if h % 2 == 0:
                dk_sums[grp, h // 2] = bank("dk", F32, 2 * P)
            for g in range(T):
                nc.tensor.matmul(
                    dk_sums[grp, h // 2][:, P * (h % 2) : P * (h % 2 + 1)],
                    lhsT=dp_neg[grp, h - h % 2][:, P * (T * (h % 2) + g) : P * (T * (h % 2) + g + 1)],
                    rhs=ident[:],
                    start=(h % 2 == 0 and g == 0),
                    stop=(h % 2 == 1 and g == T - 1),
                    is_transpose=True,
                )

        def fetch_dk(grp, half):
            dk_tokens[grp, half] = sbuf("dk_tokens", 2 * P, F32, 2)
            nc.scalar.copy(out=dk_tokens[grp, half][:], in_=dk_sums[grp, half][:])

        def turn_dk(grp, half):
            turned = bank("turn", F32, 2 * P)
            for i in range(2):
                nc.tensor.transpose(turned[:, P * i : P * (i + 1)], dk_tokens[grp, half][:, P * i : P * (i + 1)], ident[:])
            dst = dz[grp][:, BANK : 2 * BANK].rearrange("p (r h) -> p r h", h=4)[:, :, 2 * half : 2 * half + 2]
            return dst, turned[:].rearrange("p (h r) -> p r h", h=2)

        def quantize_dz(grp, s):
            if s == 0:
                dz_mx[grp] = sbuf("dz_codes", 2 * P, U32, 2), sbuf("dz_scales", 2 * P, U8, 2), E5M2
            quantize(E5M2, dz_mx[grp][0], dz_mx[grp][1], P * s, dz[grp][:, BANK * s : BANK * (s + 1)])

        def pair_dq(grp, blocks):
            nc.scalar.copy(
                out=dq_pairs[:].rearrange("p (h u r i) -> p h u r i", h=4, u=2, i=2)[:, blocks, :, 32 * grp : 32 * (grp + 1)],
                in_=dz[grp][:, 0:BANK].rearrange("p (r u i h) -> p h u r i", u=2, i=2, h=4)[:, blocks],
            )

        def pair_xm(half):
            if half == 0:
                staged["xm_pairs"] = sbuf("staged", 4096, BF16, 3)
            nc.vector.tensor_copy(
                out=staged["xm_pairs"][:].bitcast(F32).rearrange("p (c u b n f) -> p b c u n f", u=2, b=2, n=16, f=4)[:, half],
                in_=raw["xm", half][:].bitcast(F32).rearrange("p (n c f u) -> p c u n f", c=8, f=4, u=2),
            )

        def turn_words(dst, src, part, tag):
            turned = bank(tag)
            for i in range(4):
                cols = slice(P * (4 * part + i), P * (4 * part + i + 1))
                nc.tensor.transpose(turned[:, P * i : P * (i + 1)], src[:].bitcast(F32)[:, cols], ident[:])
            words = dst[:].bitcast(F32)[:, BANK * part : BANK * (part + 1)]
            return words.rearrange("p (c m u) -> p c m u", c=2, u=2), turned[:].rearrange("p (c u m) -> p c m u", c=2, u=2)

        def weave_w1(s, half):
            if half == 0:
                staged["w1", s] = sbuf("staged", 4096, BF16, 3)
            for b, engine in enumerate(("vector", "scalar")):
                copy(
                    engine,
                    staged["w1", s][:].rearrange("p (b c f m j) -> p b f m c j", b=2, c=4, f=2, j=4)[:, b, half],
                    raw["w1", 2 * s + half][:].rearrange("p (j m b c) -> p b m c j", j=4, b=2, c=4)[:, b],
                )

        def multiply_dx(grp, half, tag):
            if half == 0:
                staged["dx_tokens"] = sbuf("dx_tokens", C, F32)
            acc = bank(tag)
            for s in range(2):
                channels = slice(C * s + BANK * half, C * s + BANK * (half + 1))
                multiply_mx(acc[:], dz_mx[grp], slice(P * s, P * (s + 1)), w1_mx, channels, s == 0, s == 1)
            return staged["dx_tokens"][:, BANK * half : BANK * (half + 1)], acc[:]

        def turn_dx(half, tag):
            if half == 0:
                staged["dx"] = sbuf("dx", C, F32)
            turned = bank(tag)
            for c in range(4):
                first = BANK * half + P * c
                nc.tensor.transpose(turned[:, P * c : P * (c + 1)], staged["dx_tokens"][:, first : first + P], ident[:])
            dst = staged["dx"][:].rearrange("p (n b c f) -> p b n c f", b=2, c=4, f=T)[:, half]
            return dst, turned[:].rearrange("p (c n f) -> p n c f", c=4, f=T)

        def store_dx(grp):
            nc.sync.dma_start(
                out=out_0[GROUP * grp : GROUP * (grp + 1)].rearrange("n (m c) f -> m n (c f)", c=8),
                in_=staged["dx"][:].rearrange("p (n w) -> p n w", n=GROUP),
            )

        def quantize_dq(part):
            quantize(E5M2, dq_mx[0], dq_mx[1], 256 * part, dq_tokens[:, 1024 * part : 1024 * (part + 1)])

        def multiply_dwq(h):
            if h % 2 == 0:
                staged["dwq"] = sbuf("staged", 2 * C, F32, 3)
            rows = staged["dwq"][:, C * (h % 2) : C * (h % 2 + 1)]
            for half, engine in enumerate(("scalar", "vector")):
                acc = bank("dd")
                multiply_mx(acc[:], dq_mx, slice(P * h, P * (h + 1)), xm_mx, slice(BANK * half, BANK * (half + 1)), True, True)
                copy(
                    engine,
                    rows.rearrange("p (m b c) -> p b m c", b=2, c=4)[:, half],
                    acc[:].rearrange("p (c m) -> p m c", c=4),
                )
            nc.sync.dma_start(out=out_1.rearrange("(m h) c -> m h c", h=4)[:, h, :], in_=rows)

        everything, vector_share, scalar_share = slice(0, T), slice(0, VECTOR_FRAMES), slice(VECTOR_FRAMES, T)
        sort_k(0)
        for step in range(4):
            subtract(step, nc.vector)
        for s in range(2):
            weave_wr(s)
            load_next()
        for n in range(2):
            for s in range(2):
                weave_go(0, n, s, "vector", everything)
            load_next()
            activate(n, ACT.Tanh)
        for s in range(2):
            quantize(E4M3, wr_mx[0], wr_mx[1], BANK * s, staged["wr"][:, 2048 * s : 2048 * (s + 1)])
            quantize_go(0, s)
            copy("scalar", *weave_go_by_matmul(1, s))
            activate(s, ACT.Square)
        multiply_dd(0)
        for s in range(2):
            weave_go(1, 1, s, "vector", everything)
        for s in range(2):
            load_next()
            quantize_go(1, s)
        activate(2, ACT.Tanh)
        waiting = [weave_go_by_matmul(2, 0)]
        weave_go(2, 1, 0, "scalar", everything)
        load_saved(1)

        last = GROUPS - 1
        for step in range(ALL_STEPS):
            grp, r = divmod(step, STEPS)
            to_weave, s = divmod(step + 5, 2)
            extra = step - EXTRAS
            for move in waiting:
                copy("scalar", *move)
            waiting.clear()
            if grp > 0 and r == 5:
                store_dx(grp - 1)
            scale_dd(step)
            if step + 1 < ALL_STEPS:
                multiply_dd(step + 1)
            if step > 0:
                round_dq(step - 1)
            if grp > 0 and r in (0, 2):
                fetch_dk(grp - 1, r // 2)
            if to_weave < COUPLES:
                weave_go(to_weave, 1, s, "scalar", scalar_share)
            if step + 2 < ALL_STEPS:
                activate(step + 2, ACT.Square)
            if step == ALL_STEPS - 2:
                pair_dq(last, slice(0, 2))
            if r >= 6:
                add_dk(grp, r - 6)
            if grp > 0 and r < 2:
                add_dk(grp - 1, r + 2)
            if grp > 0 and r in (0, 2):
                waiting.append(turn_dk(grp - 1, r // 2))
            if step == ALL_STEPS - 2:
                waiting.append(turn_words(dq_tokens, dq_pairs, 0, "turn"))
            if step + 3 < ALL_STEPS:
                activate(step + 3, ACT.Tanh)
            if step + 4 < 2 * COUPLES:
                quantize_go((step + 4) // 2, step % 2)
            if to_weave < COUPLES:
                weave_go(to_weave, 1, s, "vector", vector_share)
                waiting.append(weave_go_by_matmul(to_weave, s))
                if s == 1:
                    load_next()
                    load_next()
            if grp > 0 and r == 1:
                pair_dq(grp - 1, slice(0, 4))
            if grp > 0 and r in (1, 3):
                quantize_dz(grp - 1, r // 2)
            if r == 2 and grp < last:
                sort_k(grp + 1)
            if r == 4 and grp + 1 < last:
                load_saved(grp + 2)
            if extra in (3, 5):
                half = extra // 2 - 1
                quantize(E4M3, w1_mx[0], w1_mx[1], 1024 * half, staged["w1", half][:])
            if 0 <= extra < 4:
                weave_w1(extra // 2, extra % 2)
                load_next()
            if extra in (4, 5):
                pair_xm(extra - 4)
                load_next()
            if extra == 7:
                staged["xm"] = sbuf("staged", 4096, BF16, 3)
            if 7 <= extra < 11:
                waiting.append(turn_words(staged["xm"], staged["xm_pairs"], extra - 7, "turn"))
            if extra in (12, 13):
                half = extra - 12
                quantize(E4M3, xm_mx[0], xm_mx[1], BANK * half, staged["xm"][:, 2048 * half : 2048 * (half + 1)])
            if step == ALL_STEPS - 1:
                quantize_dq(0)
            if step + 4 < ALL_STEPS:
                subtract(step + 4, nc.gpsimd)
            if grp > 0 and r == 3:
                waiting.extend(multiply_dx(grp - 1, half, "dk") for half in range(2))
            if grp > 0 and r == 4:
                waiting.extend(turn_dx(half, "dk") for half in range(2))

        round_dq(ALL_STEPS - 1)
        fetch_dk(last, 0)
        multiply_dwq(0)
        pair_dq(last, slice(2, 4))
        add_dk(last, 2)
        copy("scalar", *turn_dk(last, 0))
        copy("scalar", *turn_words(dq_tokens, dq_pairs, 1, "weave"))
        add_dk(last, 3)
        quantize_dz(last, 0)
        quantize_dq(1)
        fetch_dk(last, 1)
        multiply_dwq(1)
        copy("scalar", *turn_dk(last, 1))
        quantize_dz(last, 1)
        multiply_dwq(2)
        for half, engine in enumerate(("scalar", "vector")):
            copy(engine, *multiply_dx(last, half, "dk"))
        multiply_dwq(3)
        for half, engine in enumerate(("scalar", "vector")):
            copy(engine, *turn_dx(half, ("weave", "turn")[half]))
        store_dx(last)
